import numpy as np
import ml_dtypes


def mxq(x, axis, fmt="e4m3"):
    dtype, down = {"e4m3": (ml_dtypes.float8_e4m3fn, 7), "e5m2": (ml_dtypes.float8_e5m2, 14)}[fmt]
    v = np.moveaxis(np.asarray(x, np.float32).astype(ml_dtypes.bfloat16).astype(np.float64), axis, -1)
    blocks = v.reshape(v.shape[:-1] + (-1, 32))
    amax = np.abs(blocks).max(-1, keepdims=True)
    byte = np.maximum(np.where(amax > 0, np.frexp(amax)[1] - 1 + 127, 0) - down, 1)
    scale = np.exp2(byte - 127.0)
    codes = (blocks / scale).astype(np.float32).astype(dtype).astype(np.float64)
    return np.moveaxis((codes * scale).reshape(v.shape), -1, axis)


WIDE = False


def mx_kscale(k):
    if not WIDE:
        return np.ones(k)
    levels = np.array([10, -10, 5, -5, 0])
    a = np.random.permutation(np.resize(levels, k // 512 * 4)).reshape(k // 512, 4)
    idx = np.arange(k)
    return np.exp2(a[idx // 512, idx % 128 // 32])


BF16 = ml_dtypes.bfloat16


def bf(x):
    return np.asarray(x, np.float32).astype(BF16)


def f64(x):
    return np.asarray(x).astype(np.float64)


E2M1 = np.array([0.0, 0.5, 1.0, 1.5, 2.0, 3.0, 4.0, 6.0, -0.0, -0.5, -1.0, -1.5, -2.0, -3.0, -4.0, -6.0])


def pack_weight(w, fmt):
    k, n = w.shape
    w = f64(bf(w)).reshape(k // 32, 32, n)
    amax = np.abs(w).max(1)
    if fmt == "e4m3":
        byte = np.frexp(amax)[1] - 1 + 127 - 7
    else:
        mant, ex = np.frexp(amax / 6.0)
        byte = np.where(mant > 0.5, ex, ex - 1) + 127
    byte = np.clip(np.where(amax > 0, byte, 1), 1, 254)
    scaled = (w * np.exp2(127.0 - byte)[:, None, :]).reshape(k, n).astype(np.float32)
    by_word = np.ascontiguousarray(scaled.reshape(k // 512, 128, 4, n).transpose(0, 1, 3, 2))
    if fmt == "e4m3":
        words = by_word.astype(ml_dtypes.float8_e4m3fn).view(np.uint8)
    else:
        c = by_word.astype(ml_dtypes.float4_e2m1fn).view(np.uint8) & 0xF
        words = c[..., 0::2] | (c[..., 1::2] << 4)
    return np.ascontiguousarray(words), np.ascontiguousarray(byte.astype(np.uint8).reshape(k // 512, 16, n))


def unpack_weight(words, scales, fmt):
    g, p, n, _ = words.shape
    if fmt == "e4m3":
        vals = np.ascontiguousarray(words).view(ml_dtypes.float8_e4m3fn).astype(np.float64)
    else:
        nib = np.empty((g, p, n, 4), np.uint8)
        nib[..., 0::2] = words & 0xF
        nib[..., 1::2] = words >> 4
        vals = E2M1[nib]
    vals = vals * np.repeat(np.exp2(scales.astype(np.float64) - 127.0), 8, axis=1)[..., None]
    return vals.transpose(0, 1, 3, 2).reshape(g * 512, n)

def pack4(w):
    words, scales = pack_weight(w, "e2m1")
    return words.reshape(words.shape[0], 128, -1), scales


def unpack4(words, scales):
    return unpack_weight(words.reshape(words.shape[0], 128, -1, 2), scales, "e2m1")


B, S, E, H = 4, 2048, 512, 4
D = E // H
LN_EPS = 1e-6


def setup_inputs():
    s = mx_kscale(E)
    h_attn = bf(np.random.standard_normal((B, H, S, D)) * 0.4 * s.reshape(H, 1, D))
    x = bf(np.random.standard_normal((B, S, E)))
    out_w_words, out_w_scales = pack4(np.random.standard_normal((E, E)) * 2.0 / np.sqrt(E) / s[:, None])
    ln_gamma = bf(1.0 + 0.1 * np.random.standard_normal(E))
    ln_beta = bf(0.1 * np.random.standard_normal(E))
    return {"h_attn": h_attn,
            "x": x,
            "out_w_words": out_w_words,
            "out_w_scales": out_w_scales,
            "ln_gamma": ln_gamma,
            "ln_beta": ln_beta}


def reference(h_attn, x, out_w_words, out_w_scales, ln_gamma, ln_beta):
    merged = f64(h_attn).transpose(0, 2, 1, 3).reshape(B, S, E)
    out = mxq(merged, 2, "e4m3") @ unpack4(out_w_words, out_w_scales)
    y = out + f64(x)
    mean = y.mean(-1, keepdims=True)
    var = np.square(y - mean).mean(-1, keepdims=True)
    return (y - mean) / np.sqrt(var + LN_EPS) * f64(ln_gamma) + f64(ln_beta)

@@ -1,0 +1,232 @@
+from contextlib import ExitStack
+
+import concourse.mybir as mybir
+from concourse.masks import make_identity
+
+F32 = mybir.dt.float32
+BF16 = mybir.dt.bfloat16
+I32 = mybir.dt.int32
+U32 = mybir.dt.uint32
+U8 = mybir.dt.uint8
+FP8X4 = mybir.dt.float8_e4m3fn_x4
+FP4X4 = mybir.dt.float4_e2m1fn_x4
+ALU = mybir.AluOpType
+ACT = mybir.ActivationFunctionType
+
+B, H, S, D = 4, 4, 2048, 128
+E = H * D
+P = 128
+PACK = 4
+LN_EPS = 1e-6
+
+QUAD = 4
+QUAD_TOKENS = P * QUAD
+N_QUADS = B * S // QUAD_TOKENS
+PAIR = 2
+LOADS_AHEAD = 6
+
+FLOPS = 2 * B * S * E * E
+
+
+def tile_selfattention_pa_t_kernel(tc, h_attn, x, out_w_words, out_w_scales, ln_gamma, ln_beta, out):
+    nc = tc.nc
+    with ExitStack() as ctx:
+        ctx.enter_context(tc.manual_schedule())
+        keep = ctx.enter_context(tc.tile_pool(name="keep", bufs=1))
+        heads_in = ctx.enter_context(tc.tile_pool(name="heads_in", bufs=LOADS_AHEAD - 1))
+        resid_in = ctx.enter_context(tc.tile_pool(name="resid_in", bufs=LOADS_AHEAD + 1))
+        work = ctx.enter_context(tc.tile_pool(name="work", bufs=2))
+        sums_rows = ctx.enter_context(tc.tile_pool(name="sums_rows", bufs=3))
+        out_rows = ctx.enter_context(tc.tile_pool(name="out_rows", bufs=4))
+        stats = ctx.enter_context(tc.tile_pool(name="stats", bufs=4))
+        gamma_bank = ctx.enter_context(tc.psum_pool(name="gamma_bank", bufs=1))
+        flip_banks = ctx.enter_context(tc.psum_pool(name="flip_banks", bufs=3))
+        acc_banks = ctx.enter_context(tc.psum_pool(name="acc_banks", bufs=4))
+
+        merged_of, resid_of, flipped_of, grouped_of, codes_of, plane_of = {}, {}, {}, {}, {}, {}
+        acc_of, y_of, neg_mean_of, std_of, rstd_of, t_of = {}, {}, {}, {}, {}, {}
+
+        def live(i):
+            return 0 <= i < N_QUADS
+
+        def token_rows(dram_2d, i):
+            b, s0 = divmod(i * QUAD_TOKENS, S)
+            return dram_2d[b, s0 : s0 + QUAD_TOKENS, :].rearrange("(p a) e -> p a e", a=QUAD)
+
+        def load(i):
+            b, s0 = divmod(i * QUAD_TOKENS, S)
+            merged = heads_in.tile([P, QUAD, E], BF16, name="merged")
+            for h in range(H):
+                nc.sync.dma_start(
+                    out=merged[:, :, h * D : (h + 1) * D],
+                    in_=h_attn[b, h, s0 : s0 + QUAD_TOKENS, :].rearrange("(p a) d -> p a d", a=QUAD),
+                )
+            resid = resid_in.tile([P, QUAD, E], BF16, name="resid")
+            nc.sync.dma_start(out=resid[:], in_=token_rows(x, i))
+            merged_of[i], resid_of[i] = merged, resid
+
+        def flip(i):
+            words = merged_of[i][:].bitcast(F32)
+            flipped_of[i] = []
+            for pair in range(QUAD // PAIR):
+                flipped = flip_banks.tile([P, PAIR, 2, P], F32, name="flipped")
+                for a in range(PAIR):
+                    for u in range(2):
+                        nc.tensor.transpose(flipped[:, a, u, :], words[:, pair * PAIR + a, u : E // 2 : 2], ident[:])
+                flipped_of[i].append(flipped)
+
+        def regroup(i):
+            grouped = work.tile([P, QUAD, P, PACK], BF16, align_bytes=64, name="grouped")
+            grouped_words = grouped[:].bitcast(F32)
+            for pair in range(QUAD // PAIR):
+                nc.scalar.copy(
+                    out=grouped_words[:, pair * PAIR : (pair + 1) * PAIR, :, :],
+                    in_=flipped_of[i][pair][:].rearrange("p a u n -> p a n u"),
+                )
+            grouped_of[i] = grouped
+
+        def quantise(i):
+            codes = work.tile([P, QUAD * P], U32, align_bytes=64, name="codes")
+            plane = work.tile([P, QUAD * P], U8, align_bytes=64, name="plane")
+            nc.vector.quantize_mx(
+                out=codes[:].bitcast(FP8X4),
+                scales=plane[:],
+                in_=grouped_of[i][:].rearrange("p a n t -> p (a n t)"),
+            )
+            codes_of[i], plane_of[i] = codes, plane
+
+        def project(i):
+            acc_of[i] = []
+            for a in range(QUAD):
+                acc = acc_banks.tile([P, E], F32, name="acc")
+                nc.tensor.matmul_mx(
+                    out=acc[:],
+                    lhsT=codes_of[i][:, a * P : (a + 1) * P].bitcast(FP8X4),
+                    lhsT_scale=plane_of[i][:, a * P : (a + 1) * P],
+                    rhs=w_words[:].bitcast(FP4X4),
+                    rhs_scale=w_plane[:],
+                    start=True,
+                    stop=True,
+                )
+                acc_of[i].append(acc)
+
+        def add_residual(i):
+            y = sums_rows.tile([P, QUAD, E], F32, name="y")
+            sums = stats.tile([P, QUAD], F32, name="sums")
+            for a in range(QUAD):
+                nc.vector.scalar_tensor_tensor(
+                    out=y[:, a, :],
+                    in0=acc_of[i][a][:],
+                    scalar=1.0,
+                    in1=resid_of[i][:, a, :],
+                    op0=ALU.mult,
+                    op1=ALU.add,
+                    accum_out=sums[:, a : a + 1],
+                )
+            neg_mean = stats.tile([P, QUAD], F32, name="neg_mean")
+            nc.vector.tensor_scalar_mul(out=neg_mean[:], in0=sums[:], scalar1=-1.0 / E)
+            y_of[i], neg_mean_of[i] = y, neg_mean
+
+        def deviation(i):
+            squares = work.tile([P, QUAD, E], BF16, name="squares")
+            sum_sq = stats.tile([P, QUAD], F32, name="sum_sq")
+            for a in range(QUAD):
+                nc.scalar.activation(
+                    out=squares[:, a, :],
+                    in_=y_of[i][:, a, :],
+                    func=ACT.Square,
+                    bias=neg_mean_of[i][:, a : a + 1],
+                    scale=1.0,
+                    accum_out=sum_sq[:, a : a + 1],
+                )
+            std = stats.tile([P, QUAD], F32, name="std")
+            nc.scalar.activation(out=std[:], in_=sum_sq[:], func=ACT.Sqrt, bias=eps[:], scale=1.0 / E)
+            std_of[i] = std
+
+        def invert(i):
+            rstd = stats.tile([P, QUAD], F32, name="rstd")
+            nc.vector.reciprocal(out=rstd[:], in_=std_of[i][:])
+            rstd_of[i] = rstd
+
+        def centre_and_gain(i):
+            t = out_rows.tile([P, QUAD, E], F32, name="t")
+            for a in range(QUAD):
+                nc.vector.scalar_tensor_tensor(
+                    out=t[:, a, :],
+                    in0=y_of[i][:, a, :],
+                    scalar=neg_mean_of[i][:, a : a + 1],
+                    in1=gamma_all[:],
+                    op0=ALU.add,
+                    op1=ALU.mult,
+                )
+            t_of[i] = t
+
+        def scale_offset_store(i):
+            t, rstd = t_of[i], rstd_of[i]
+            nc.gpsimd.tensor_scalar(
+                out=t[:, 0, :], in0=t[:, 0, :], scalar1=rstd[:, 0:1], scalar2=0.0, op0=ALU.mult, op1=ALU.add
+            )
+            for a in range(1, QUAD):
+                nc.scalar.activation(out=t[:, a, :], in_=t[:, a, :], func=ACT.Copy, scale=rstd[:, a : a + 1])
+            for pair in range(QUAD // PAIR):
+                both = slice(pair * PAIR, (pair + 1) * PAIR)
+                nc.gpsimd.tensor_tensor(
+                    out=t[:, both, :],
+                    in0=t[:, both, :],
+                    in1=beta_all[:].unsqueeze(1).to_broadcast([P, PAIR, E]),
+                    op=ALU.add,
+                )
+                nc.sync.dma_start(out=token_rows(out, i)[:, both, :], in_=t[:, both, :])
+
+        w_plane = keep.tile([P, E], U8, align_bytes=64)
+        nc.vector.memset(w_plane[:].bitcast(I32), 0)
+        gain_rows = keep.tile([P, 2, E], BF16)
+        nc.vector.memset(gain_rows[:], 0.0)
+        ones = keep.tile([P, P], BF16)
+        nc.vector.memset(ones[:], 1.0)
+        eps = keep.tile([P, 1], F32)
+        nc.vector.memset(eps[:], LN_EPS)
+        ident = keep.tile([P, P], F32)
+        make_identity(nc, ident[:])
+        warm = keep.tile([P, 1], F32)
+        nc.scalar.activation(out=warm[:], in_=eps[:], func=ACT.Sqrt)
+
+        load(0)
+        nc.sync.dma_start(out=gain_rows[0:1, 0, :], in_=ln_gamma.unsqueeze(0))
+        nc.sync.dma_start(out=gain_rows[0:1, 1, :], in_=ln_beta.unsqueeze(0))
+        w_words = keep.tile([P, 2 * E], U8, align_bytes=64)
+        nc.sync.dma_start(out=w_words[:].bitcast(I32), in_=out_w_words[0].bitcast(I32))
+        for quadrant in range(4):
+            nc.sync.dma_start(
+                out=w_plane[32 * quadrant : 32 * quadrant + 4, :].bitcast(I32),
+                in_=out_w_scales[0, 4 * quadrant : 4 * quadrant + 4, :].bitcast(I32),
+            )
+        for i in range(1, LOADS_AHEAD):
+            load(i)
+
+        gamma_all = gamma_bank.tile([P, E], F32)
+        nc.tensor.matmul(out=gamma_all[:], lhsT=ones[:], rhs=gain_rows[:, 0, :], start=True, stop=True)
+        beta_psum = acc_banks.tile([P, E], F32, name="acc")
+        nc.tensor.matmul(out=beta_psum[:], lhsT=ones[:], rhs=gain_rows[:, 1, :], start=True, stop=True)
+        beta_all = keep.tile([P, E], F32)
+        nc.scalar.copy(out=beta_all[:], in_=beta_psum[:])
+
+        for n in range(-2, N_QUADS + 2):
+            if n >= 0 and live(n + LOADS_AHEAD):
+                load(n + LOADS_AHEAD)
+            if live(n + 2):
+                flip(n + 2)
+            if live(n):
+                add_residual(n)
+            if live(n + 1):
+                quantise(n + 1)
+                project(n + 1)
+            if live(n - 1):
+                deviation(n - 1)
+                invert(n - 1)
+            if live(n):
+                centre_and_gain(n)
+            if live(n + 2):
+                regroup(n + 2)
+            if live(n - 1):
+                scale_offset_store(n - 1)

@@ -44,7 +44,7 @@ def tile_selfattention_pa_t_kernel(tc, h_attn, x, out_w_words, out_w_scales, ln_
         acc_banks = ctx.enter_context(tc.psum_pool(name="acc_banks", bufs=4))
 
         merged_of, resid_of, flipped_of, grouped_of, codes_of, plane_of = {}, {}, {}, {}, {}, {}
-        acc_of, y_of, neg_mean_of, std_of, rstd_of, t_of = {}, {}, {}, {}, {}, {}
+        acc_of, y_of, sums_of, neg_mean_of, std_of, rstd_of, t_of = {}, {}, {}, {}, {}, {}, {}
 
         def live(i):
             return 0 <= i < N_QUADS
@@ -123,9 +123,12 @@ def tile_selfattention_pa_t_kernel(tc, h_attn, x, out_w_words, out_w_scales, ln_
                     op1=ALU.add,
                     accum_out=sums[:, a : a + 1],
                 )
+            y_of[i], sums_of[i] = y, sums
+
+        def negate_mean(i):
             neg_mean = stats.tile([P, QUAD], F32, name="neg_mean")
-            nc.vector.tensor_scalar_mul(out=neg_mean[:], in0=sums[:], scalar1=-1.0 / E)
-            y_of[i], neg_mean_of[i] = y, neg_mean
+            nc.vector.tensor_scalar_mul(out=neg_mean[:], in0=sums_of[i][:], scalar1=-1.0 / E)
+            neg_mean_of[i] = neg_mean
 
         def deviation(i):
             squares = work.tile([P, QUAD, E], BF16, name="squares")
@@ -163,10 +166,7 @@ def tile_selfattention_pa_t_kernel(tc, h_attn, x, out_w_words, out_w_scales, ln_
 
         def scale_offset_store(i):
             t, rstd = t_of[i], rstd_of[i]
-            nc.gpsimd.tensor_scalar(
-                out=t[:, 0, :], in0=t[:, 0, :], scalar1=rstd[:, 0:1], scalar2=0.0, op0=ALU.mult, op1=ALU.add
-            )
-            for a in range(1, QUAD):
+            for a in range(QUAD):
                 nc.scalar.activation(out=t[:, a, :], in_=t[:, a, :], func=ACT.Copy, scale=rstd[:, a : a + 1])
             for pair in range(QUAD // PAIR):
                 both = slice(pair * PAIR, (pair + 1) * PAIR)
@@ -216,17 +216,20 @@ def tile_selfattention_pa_t_kernel(tc, h_attn, x, out_w_words, out_w_scales, ln_
                 load(n + LOADS_AHEAD)
             if live(n + 2):
                 flip(n + 2)
+            if live(n - 1):
+                deviation(n - 1)
+            if live(n + 2):
+                regroup(n + 2)
             if live(n):
                 add_residual(n)
+            if live(n - 1):
+                invert(n - 1)
+            if live(n):
+                negate_mean(n)
             if live(n + 1):
                 quantise(n + 1)
                 project(n + 1)
-            if live(n - 1):
-                deviation(n - 1)
-                invert(n - 1)
             if live(n):
                 centre_and_gain(n)
-            if live(n + 2):
-                regroup(n + 2)
             if live(n - 1):
                 scale_offset_store(n - 1)

@@ -23,7 +23,9 @@ QUAD = 4
 QUAD_TOKENS = P * QUAD
 N_QUADS = B * S // QUAD_TOKENS
 PAIR = 2
-LOADS_AHEAD = 6
+HEADS_AHEAD = 6
+RESID_AHEAD = 4
+VECTOR_TAIL = 2
 
 FLOPS = 2 * B * S * E * E
 
@@ -33,14 +35,14 @@ def tile_selfattention_pa_t_kernel(tc, h_attn, x, out_w_words, out_w_scales, ln_
     with ExitStack() as ctx:
         ctx.enter_context(tc.manual_schedule())
         keep = ctx.enter_context(tc.tile_pool(name="keep", bufs=1))
-        heads_in = ctx.enter_context(tc.tile_pool(name="heads_in", bufs=LOADS_AHEAD - 1))
-        resid_in = ctx.enter_context(tc.tile_pool(name="resid_in", bufs=LOADS_AHEAD + 1))
+        heads_in = ctx.enter_context(tc.tile_pool(name="heads_in", bufs=HEADS_AHEAD - 1))
+        resid_in = ctx.enter_context(tc.tile_pool(name="resid_in", bufs=RESID_AHEAD + 1))
         work = ctx.enter_context(tc.tile_pool(name="work", bufs=2))
         sums_rows = ctx.enter_context(tc.tile_pool(name="sums_rows", bufs=3))
         out_rows = ctx.enter_context(tc.tile_pool(name="out_rows", bufs=4))
         stats = ctx.enter_context(tc.tile_pool(name="stats", bufs=4))
-        gamma_bank = ctx.enter_context(tc.psum_pool(name="gamma_bank", bufs=1))
-        flip_banks = ctx.enter_context(tc.psum_pool(name="flip_banks", bufs=3))
+        gain_banks = ctx.enter_context(tc.psum_pool(name="gain_banks", bufs=1))
+        flip_banks = ctx.enter_context(tc.psum_pool(name="flip_banks", bufs=2))
         acc_banks = ctx.enter_context(tc.psum_pool(name="acc_banks", bufs=4))
 
         merged_of, resid_of, flipped_of, grouped_of, codes_of, plane_of = {}, {}, {}, {}, {}, {}
@@ -53,7 +55,7 @@ def tile_selfattention_pa_t_kernel(tc, h_attn, x, out_w_words, out_w_scales, ln_
             b, s0 = divmod(i * QUAD_TOKENS, S)
             return dram_2d[b, s0 : s0 + QUAD_TOKENS, :].rearrange("(p a) e -> p a e", a=QUAD)
 
-        def load(i):
+        def load_heads(i):
             b, s0 = divmod(i * QUAD_TOKENS, S)
             merged = heads_in.tile([P, QUAD, E], BF16, name="merged")
             for h in range(H):
@@ -61,9 +63,12 @@ def tile_selfattention_pa_t_kernel(tc, h_attn, x, out_w_words, out_w_scales, ln_
                     out=merged[:, :, h * D : (h + 1) * D],
                     in_=h_attn[b, h, s0 : s0 + QUAD_TOKENS, :].rearrange("(p a) d -> p a d", a=QUAD),
                 )
+            merged_of[i] = merged
+
+        def load_resid(i):
             resid = resid_in.tile([P, QUAD, E], BF16, name="resid")
             nc.sync.dma_start(out=resid[:], in_=token_rows(x, i))
-            merged_of[i], resid_of[i] = merged, resid
+            resid_of[i] = resid
 
         def flip(i):
             words = merged_of[i][:].bitcast(F32)
@@ -178,42 +183,26 @@ def tile_selfattention_pa_t_kernel(tc, h_attn, x, out_w_words, out_w_scales, ln_
                 )
                 nc.sync.dma_start(out=token_rows(out, i)[:, both, :], in_=t[:, both, :])
 
-        w_plane = keep.tile([P, E], U8, align_bytes=64)
-        nc.vector.memset(w_plane[:].bitcast(I32), 0)
-        gain_rows = keep.tile([P, 2, E], BF16)
-        nc.vector.memset(gain_rows[:], 0.0)
-        ones = keep.tile([P, P], BF16)
-        nc.vector.memset(ones[:], 1.0)
-        eps = keep.tile([P, 1], F32)
-        nc.vector.memset(eps[:], LN_EPS)
-        ident = keep.tile([P, P], F32)
-        make_identity(nc, ident[:])
-        warm = keep.tile([P, 1], F32)
-        nc.scalar.activation(out=warm[:], in_=eps[:], func=ACT.Sqrt)
+        def finish_on_vector(i):
+            t, rstd = t_of[i], rstd_of[i]
+            for pair in range(QUAD // PAIR):
+                both = slice(pair * PAIR, (pair + 1) * PAIR)
+                for a in range(pair * PAIR, (pair + 1) * PAIR):
+                    nc.vector.scalar_tensor_tensor(
+                        out=t[:, a, :],
+                        in0=t[:, a, :],
+                        scalar=rstd[:, a : a + 1],
+                        in1=beta_bank[:],
+                        op0=ALU.mult,
+                        op1=ALU.add,
+                    )
+                nc.sync.dma_start(out=token_rows(out, i)[:, both, :], in_=t[:, both, :])
 
-        load(0)
-        nc.sync.dma_start(out=gain_rows[0:1, 0, :], in_=ln_gamma.unsqueeze(0))
-        nc.sync.dma_start(out=gain_rows[0:1, 1, :], in_=ln_beta.unsqueeze(0))
-        w_words = keep.tile([P, 2 * E], U8, align_bytes=64)
-        nc.sync.dma_start(out=w_words[:].bitcast(I32), in_=out_w_words[0].bitcast(I32))
-        for quadrant in range(4):
-            nc.sync.dma_start(
-                out=w_plane[32 * quadrant : 32 * quadrant + 4, :].bitcast(I32),
-                in_=out_w_scales[0, 4 * quadrant : 4 * quadrant + 4, :].bitcast(I32),
-            )
-        for i in range(1, LOADS_AHEAD):
-            load(i)
-
-        gamma_all = gamma_bank.tile([P, E], F32)
-        nc.tensor.matmul(out=gamma_all[:], lhsT=ones[:], rhs=gain_rows[:, 0, :], start=True, stop=True)
-        beta_psum = acc_banks.tile([P, E], F32, name="acc")
-        nc.tensor.matmul(out=beta_psum[:], lhsT=ones[:], rhs=gain_rows[:, 1, :], start=True, stop=True)
-        beta_all = keep.tile([P, E], F32)
-        nc.scalar.copy(out=beta_all[:], in_=beta_psum[:])
-
-        for n in range(-2, N_QUADS + 2):
-            if n >= 0 and live(n + LOADS_AHEAD):
-                load(n + LOADS_AHEAD)
+        def step(n):
+            if n >= 0 and live(n + HEADS_AHEAD):
+                load_heads(n + HEADS_AHEAD)
+            if n >= 0 and live(n + RESID_AHEAD):
+                load_resid(n + RESID_AHEAD)
             if live(n + 2):
                 flip(n + 2)
             if live(n - 1):
@@ -229,7 +218,52 @@ def tile_selfattention_pa_t_kernel(tc, h_attn, x, out_w_words, out_w_scales, ln_
             if live(n + 1):
                 quantise(n + 1)
                 project(n + 1)
+            if live(n - 1) and n - 1 >= N_QUADS - VECTOR_TAIL:
+                finish_on_vector(n - 1)
             if live(n):
                 centre_and_gain(n)
-            if live(n - 1):
+            if live(n - 1) and n - 1 < N_QUADS - VECTOR_TAIL:
                 scale_offset_store(n - 1)
+
+        w_plane = keep.tile([P, E], U8, align_bytes=64)
+        nc.vector.memset(w_plane[:].bitcast(I32), 0)
+        gain_rows = keep.tile([P, 2, E], BF16)
+        nc.vector.memset(gain_rows[:], 0.0)
+        ones = keep.tile([P, P], BF16)
+        nc.vector.memset(ones[:], 1.0)
+        eps = keep.tile([P, 1], F32)
+        nc.vector.memset(eps[:], LN_EPS)
+        ident = keep.tile([P, P], F32)
+        make_identity(nc, ident[:])
+        warm = keep.tile([P, 1], F32)
+        nc.scalar.activation(out=warm[:], in_=eps[:], func=ACT.Sqrt)
+
+        load_heads(0)
+        w_words = keep.tile([P, 2 * E], U8, align_bytes=64)
+        nc.sync.dma_start(out=w_words[:].bitcast(I32), in_=out_w_words[0].bitcast(I32))
+        for quadrant in range(4):
+            nc.sync.dma_start(
+                out=w_plane[32 * quadrant : 32 * quadrant + 4, :].bitcast(I32),
+                in_=out_w_scales[0, 4 * quadrant : 4 * quadrant + 4, :].bitcast(I32),
+            )
+        load_heads(1)
+        load_resid(0)
+        nc.sync.dma_start(out=gain_rows[0:1, 0, :], in_=ln_gamma.unsqueeze(0))
+        nc.sync.dma_start(out=gain_rows[0:1, 1, :], in_=ln_beta.unsqueeze(0))
+        for i in range(2, HEADS_AHEAD):
+            load_heads(i)
+            if i - 1 < RESID_AHEAD:
+                load_resid(i - 1)
+
+        for n in range(-2, 0):
+            step(n)
+
+        gamma_all = gain_banks.tile([P, E], F32)
+        nc.tensor.matmul(out=gamma_all[:], lhsT=ones[:], rhs=gain_rows[:, 0, :], start=True, stop=True)
+        beta_bank = gain_banks.tile([P, E], F32)
+        nc.tensor.matmul(out=beta_bank[:], lhsT=ones[:], rhs=gain_rows[:, 1, :], start=True, stop=True)
+        beta_all = keep.tile([P, E], F32)
+        nc.scalar.copy(out=beta_all[:], in_=beta_bank[:])
+
+        for n in range(0, N_QUADS + 2):
+            step(n)

@@ -175,12 +175,8 @@ def tile_selfattention_pa_t_kernel(tc, h_attn, x, out_w_words, out_w_scales, ln_
                 nc.scalar.activation(out=t[:, a, :], in_=t[:, a, :], func=ACT.Copy, scale=rstd[:, a : a + 1])
             for pair in range(QUAD // PAIR):
                 both = slice(pair * PAIR, (pair + 1) * PAIR)
-                nc.gpsimd.tensor_tensor(
-                    out=t[:, both, :],
-                    in0=t[:, both, :],
-                    in1=beta_all[:].unsqueeze(1).to_broadcast([P, PAIR, E]),
-                    op=ALU.add,
-                )
+                for a in range(pair * PAIR, (pair + 1) * PAIR):
+                    nc.gpsimd.tensor_tensor(out=t[:, a, :], in0=t[:, a, :], in1=beta_all[:], op=ALU.add)
                 nc.sync.dma_start(out=token_rows(out, i)[:, both, :], in_=t[:, both, :])
 
         def finish_on_vector(i):

@@ -23,7 +23,7 @@ QUAD = 4
 QUAD_TOKENS = P * QUAD
 N_QUADS = B * S // QUAD_TOKENS
 PAIR = 2
-HEADS_AHEAD = 6
+HEADS_AHEAD = 7
 RESID_AHEAD = 4
 VECTOR_TAIL = 2
 
@@ -35,9 +35,10 @@ def tile_selfattention_pa_t_kernel(tc, h_attn, x, out_w_words, out_w_scales, ln_
     with ExitStack() as ctx:
         ctx.enter_context(tc.manual_schedule())
         keep = ctx.enter_context(tc.tile_pool(name="keep", bufs=1))
-        heads_in = ctx.enter_context(tc.tile_pool(name="heads_in", bufs=HEADS_AHEAD - 1))
+        heads_in = ctx.enter_context(tc.tile_pool(name="heads_in", bufs=HEADS_AHEAD - 2))
         resid_in = ctx.enter_context(tc.tile_pool(name="resid_in", bufs=RESID_AHEAD + 1))
         work = ctx.enter_context(tc.tile_pool(name="work", bufs=2))
+        grouped_rows = ctx.enter_context(tc.tile_pool(name="grouped_rows", bufs=3))
         sums_rows = ctx.enter_context(tc.tile_pool(name="sums_rows", bufs=3))
         out_rows = ctx.enter_context(tc.tile_pool(name="out_rows", bufs=4))
         stats = ctx.enter_context(tc.tile_pool(name="stats", bufs=4))
@@ -46,7 +47,7 @@ def tile_selfattention_pa_t_kernel(tc, h_attn, x, out_w_words, out_w_scales, ln_
         acc_banks = ctx.enter_context(tc.psum_pool(name="acc_banks", bufs=4))
 
         merged_of, resid_of, flipped_of, grouped_of, codes_of, plane_of = {}, {}, {}, {}, {}, {}
-        acc_of, y_of, sums_of, neg_mean_of, std_of, rstd_of, t_of = {}, {}, {}, {}, {}, {}, {}
+        acc_of, y_of, sums_of, neg_mean_of, rstd_of, t_of = {}, {}, {}, {}, {}, {}
 
         def live(i):
             return 0 <= i < N_QUADS
@@ -81,7 +82,7 @@ def tile_selfattention_pa_t_kernel(tc, h_attn, x, out_w_words, out_w_scales, ln_
                 flipped_of[i].append(flipped)
 
         def regroup(i):
-            grouped = work.tile([P, QUAD, P, PACK], BF16, align_bytes=64, name="grouped")
+            grouped = grouped_rows.tile([P, QUAD, P, PACK], BF16, align_bytes=64, name="grouped")
             grouped_words = grouped[:].bitcast(F32)
             for pair in range(QUAD // PAIR):
                 nc.scalar.copy(
@@ -132,7 +133,7 @@ def tile_selfattention_pa_t_kernel(tc, h_attn, x, out_w_words, out_w_scales, ln_
 
         def negate_mean(i):
             neg_mean = stats.tile([P, QUAD], F32, name="neg_mean")
-            nc.vector.tensor_scalar_mul(out=neg_mean[:], in0=sums_of[i][:], scalar1=-1.0 / E)
+            nc.scalar.activation(out=neg_mean[:], in_=sums_of[i][:], func=ACT.Copy, scale=-1.0 / E)
             neg_mean_of[i] = neg_mean
 
         def deviation(i):
@@ -147,13 +148,8 @@ def tile_selfattention_pa_t_kernel(tc, h_attn, x, out_w_words, out_w_scales, ln_
                     scale=1.0,
                     accum_out=sum_sq[:, a : a + 1],
                 )
-            std = stats.tile([P, QUAD], F32, name="std")
-            nc.scalar.activation(out=std[:], in_=sum_sq[:], func=ACT.Sqrt, bias=eps[:], scale=1.0 / E)
-            std_of[i] = std
-
-        def invert(i):
             rstd = stats.tile([P, QUAD], F32, name="rstd")
-            nc.vector.reciprocal(out=rstd[:], in_=std_of[i][:])
+            nc.scalar.activation(out=rstd[:], in_=sum_sq[:], func=ACT.Abs_reciprocal_sqrt, bias=eps[:], scale=1.0 / E)
             rstd_of[i] = rstd
 
         def centre_and_gain(i):
@@ -173,11 +169,16 @@ def tile_selfattention_pa_t_kernel(tc, h_attn, x, out_w_words, out_w_scales, ln_
             t, rstd = t_of[i], rstd_of[i]
             for a in range(QUAD):
                 nc.scalar.activation(out=t[:, a, :], in_=t[:, a, :], func=ACT.Copy, scale=rstd[:, a : a + 1])
-            for pair in range(QUAD // PAIR):
-                both = slice(pair * PAIR, (pair + 1) * PAIR)
-                for a in range(pair * PAIR, (pair + 1) * PAIR):
-                    nc.gpsimd.tensor_tensor(out=t[:, a, :], in0=t[:, a, :], in1=beta_all[:], op=ALU.add)
-                nc.sync.dma_start(out=token_rows(out, i)[:, both, :], in_=t[:, both, :])
+            for a in range(PAIR):
+                nc.gpsimd.tensor_tensor(out=t[:, a, :], in0=t[:, a, :], in1=beta_all[:], op=ALU.add)
+            nc.sync.dma_start(out=token_rows(out, i)[:, 0:PAIR, :], in_=t[:, 0:PAIR, :])
+            nc.gpsimd.tensor_tensor(
+                out=t[:, PAIR:QUAD, :],
+                in0=t[:, PAIR:QUAD, :],
+                in1=beta_all[:].unsqueeze(1).to_broadcast([P, PAIR, E]),
+                op=ALU.add,
+            )
+            nc.sync.dma_start(out=token_rows(out, i)[:, PAIR:QUAD, :], in_=t[:, PAIR:QUAD, :])
 
         def finish_on_vector(i):
             t, rstd = t_of[i], rstd_of[i]
@@ -199,27 +200,23 @@ def tile_selfattention_pa_t_kernel(tc, h_attn, x, out_w_words, out_w_scales, ln_
                 load_heads(n + HEADS_AHEAD)
             if n >= 0 and live(n + RESID_AHEAD):
                 load_resid(n + RESID_AHEAD)
-            if live(n + 2):
-                flip(n + 2)
-            if live(n - 1):
-                deviation(n - 1)
-            if live(n + 2):
-                regroup(n + 2)
             if live(n):
                 add_residual(n)
-            if live(n - 1):
-                invert(n - 1)
-            if live(n):
                 negate_mean(n)
             if live(n + 1):
                 quantise(n + 1)
                 project(n + 1)
+            if live(n + 3):
+                flip(n + 3)
+            if live(n - 1) and n - 1 < N_QUADS - VECTOR_TAIL:
+                scale_offset_store(n - 1)
             if live(n - 1) and n - 1 >= N_QUADS - VECTOR_TAIL:
                 finish_on_vector(n - 1)
             if live(n):
                 centre_and_gain(n)
-            if live(n - 1) and n - 1 < N_QUADS - VECTOR_TAIL:
-                scale_offset_store(n - 1)
+                deviation(n)
+            if live(n + 3):
+                regroup(n + 3)
 
         w_plane = keep.tile([P, E], U8, align_bytes=64)
         nc.vector.memset(w_plane[:].bitcast(I32), 0)
@@ -232,7 +229,7 @@ def tile_selfattention_pa_t_kernel(tc, h_attn, x, out_w_words, out_w_scales, ln_
         ident = keep.tile([P, P], F32)
         make_identity(nc, ident[:])
         warm = keep.tile([P, 1], F32)
-        nc.scalar.activation(out=warm[:], in_=eps[:], func=ACT.Sqrt)
+        nc.scalar.activation(out=warm[:], in_=eps[:], func=ACT.Abs_reciprocal_sqrt)
 
         load_heads(0)
         w_words = keep.tile([P, 2 * E], U8, align_bytes=64)
@@ -251,7 +248,7 @@ def tile_selfattention_pa_t_kernel(tc, h_attn, x, out_w_words, out_w_scales, ln_
             if i - 1 < RESID_AHEAD:
                 load_resid(i - 1)
 
-        for n in range(-2, 0):
+        for n in range(-3, 0):
             step(n)
 
         gamma_all = gain_banks.tile([P, E], F32)

@@ -26,6 +26,7 @@ PAIR = 2
 HEADS_AHEAD = 7
 RESID_AHEAD = 4
 VECTOR_TAIL = 2
+VECTOR_SHARE = E // 2
 
 FLOPS = 2 * B * S * E * E
 
@@ -167,17 +168,24 @@ def tile_selfattention_pa_t_kernel(tc, h_attn, x, out_w_words, out_w_scales, ln_
 
         def scale_offset_store(i):
             t, rstd = t_of[i], rstd_of[i]
-            for a in range(QUAD):
-                nc.scalar.activation(out=t[:, a, :], in_=t[:, a, :], func=ACT.Copy, scale=rstd[:, a : a + 1])
-            for a in range(PAIR):
-                nc.gpsimd.tensor_tensor(out=t[:, a, :], in0=t[:, a, :], in1=beta_all[:], op=ALU.add)
-            nc.sync.dma_start(out=token_rows(out, i)[:, 0:PAIR, :], in_=t[:, 0:PAIR, :])
-            nc.gpsimd.tensor_tensor(
-                out=t[:, PAIR:QUAD, :],
-                in0=t[:, PAIR:QUAD, :],
-                in1=beta_all[:].unsqueeze(1).to_broadcast([P, PAIR, E]),
-                op=ALU.add,
+            last = QUAD - 1
+            kept = E - VECTOR_SHARE
+            nc.vector.scalar_tensor_tensor(
+                out=t[:, last, kept:E],
+                in0=t[:, last, kept:E],
+                scalar=rstd[:, last : last + 1],
+                in1=beta_bank[:, kept:E],
+                op0=ALU.mult,
+                op1=ALU.add,
             )
+            for a in range(last):
+                nc.scalar.activation(out=t[:, a, :], in_=t[:, a, :], func=ACT.Copy, scale=rstd[:, a : a + 1])
+            nc.scalar.activation(out=t[:, last, 0:kept], in_=t[:, last, 0:kept], func=ACT.Copy, scale=rstd[:, last : last + 1])
+            for a in range(PAIR):
+                nc.gpsimd.tensor_tensor(out=t[:, a, :], in0=t[:, a, :], in1=beta_twice[:, 0:E], op=ALU.add)
+            nc.sync.dma_start(out=token_rows(out, i)[:, 0:PAIR, :], in_=t[:, 0:PAIR, :])
+            rest = t[:, PAIR:QUAD, :].rearrange("p a e -> p (a e)")[:, 0 : E + kept]
+            nc.gpsimd.tensor_tensor(out=rest, in0=rest, in1=beta_twice[:, 0 : E + kept], op=ALU.add)
             nc.sync.dma_start(out=token_rows(out, i)[:, PAIR:QUAD, :], in_=t[:, PAIR:QUAD, :])
 
         def finish_on_vector(i):
@@ -255,8 +263,9 @@ def tile_selfattention_pa_t_kernel(tc, h_attn, x, out_w_words, out_w_scales, ln_
         nc.tensor.matmul(out=gamma_all[:], lhsT=ones[:], rhs=gain_rows[:, 0, :], start=True, stop=True)
         beta_bank = gain_banks.tile([P, E], F32)
         nc.tensor.matmul(out=beta_bank[:], lhsT=ones[:], rhs=gain_rows[:, 1, :], start=True, stop=True)
-        beta_all = keep.tile([P, E], F32)
-        nc.scalar.copy(out=beta_all[:], in_=beta_bank[:])
+        beta_twice = keep.tile([P, PAIR * E], F32)
+        for a in range(PAIR):
+            nc.scalar.copy(out=beta_twice[:, a * E : (a + 1) * E], in_=beta_bank[:])
 
         for n in range(0, N_QUADS + 2):
             step(n)

@@ -25,7 +25,6 @@ N_QUADS = B * S // QUAD_TOKENS
 PAIR = 2
 HEADS_AHEAD = 7
 RESID_AHEAD = 4
-VECTOR_TAIL = 2
 VECTOR_SHARE = E // 2
 
 FLOPS = 2 * B * S * E * E
@@ -48,7 +47,7 @@ def tile_selfattention_pa_t_kernel(tc, h_attn, x, out_w_words, out_w_scales, ln_
         acc_banks = ctx.enter_context(tc.psum_pool(name="acc_banks", bufs=4))
 
         merged_of, resid_of, flipped_of, grouped_of, codes_of, plane_of = {}, {}, {}, {}, {}, {}
-        acc_of, y_of, sums_of, neg_mean_of, rstd_of, t_of = {}, {}, {}, {}, {}, {}
+        acc_of, y_of, sums_of, neg_mean_of, sum_sq_of, rstd_of, t_of = {}, {}, {}, {}, {}, {}, {}
 
         def live(i):
             return 0 <= i < N_QUADS
@@ -120,6 +119,9 @@ def tile_selfattention_pa_t_kernel(tc, h_attn, x, out_w_words, out_w_scales, ln_
         def add_residual(i):
             y = sums_rows.tile([P, QUAD, E], F32, name="y")
             sums = stats.tile([P, QUAD], F32, name="sums")
+            neg_mean_of[i] = stats.tile([P, QUAD], F32, name="neg_mean")
+            sum_sq_of[i] = stats.tile([P, QUAD], F32, name="sum_sq")
+            rstd_of[i] = stats.tile([P, QUAD], F32, name="rstd")
             for a in range(QUAD):
                 nc.vector.scalar_tensor_tensor(
                     out=y[:, a, :],
@@ -132,30 +134,35 @@ def tile_selfattention_pa_t_kernel(tc, h_attn, x, out_w_words, out_w_scales, ln_
                 )
             y_of[i], sums_of[i] = y, sums
 
-        def negate_mean(i):
-            neg_mean = stats.tile([P, QUAD], F32, name="neg_mean")
-            nc.scalar.activation(out=neg_mean[:], in_=sums_of[i][:], func=ACT.Copy, scale=-1.0 / E)
-            neg_mean_of[i] = neg_mean
+        def negate_mean(i, tiles=slice(0, QUAD)):
+            nc.scalar.activation(out=neg_mean_of[i][:, tiles], in_=sums_of[i][:, tiles], func=ACT.Copy, scale=-1.0 / E)
 
-        def deviation(i):
-            squares = work.tile([P, QUAD, E], BF16, name="squares")
-            sum_sq = stats.tile([P, QUAD], F32, name="sum_sq")
-            for a in range(QUAD):
-                nc.scalar.activation(
-                    out=squares[:, a, :],
-                    in_=y_of[i][:, a, :],
-                    func=ACT.Square,
-                    bias=neg_mean_of[i][:, a : a + 1],
-                    scale=1.0,
-                    accum_out=sum_sq[:, a : a + 1],
-                )
-            rstd = stats.tile([P, QUAD], F32, name="rstd")
-            nc.scalar.activation(out=rstd[:], in_=sum_sq[:], func=ACT.Abs_reciprocal_sqrt, bias=eps[:], scale=1.0 / E)
-            rstd_of[i] = rstd
+        def squares_of(i, a):
+            squares = work.tile([P, E], BF16, name="squares")
+            nc.scalar.activation(
+                out=squares[:],
+                in_=y_of[i][:, a, :],
+                func=ACT.Square,
+                bias=neg_mean_of[i][:, a : a + 1],
+                scale=1.0,
+                accum_out=sum_sq_of[i][:, a : a + 1],
+            )
 
-        def centre_and_gain(i):
-            t = out_rows.tile([P, QUAD, E], F32, name="t")
-            for a in range(QUAD):
+        def inverse_deviation(i, tiles):
+            nc.scalar.activation(
+                out=rstd_of[i][:, tiles], in_=sum_sq_of[i][:, tiles], func=ACT.Abs_reciprocal_sqrt, bias=eps[:], scale=1.0 / E
+            )
+
+        def deviation(i, tiles=slice(0, QUAD)):
+            for a in range(tiles.start, tiles.stop):
+                squares_of(i, a)
+            inverse_deviation(i, tiles)
+
+        def centre_and_gain(i, tiles=(0, 1, 2, 3)):
+            if i not in t_of:
+                t_of[i] = out_rows.tile([P, QUAD, E], F32, name="t")
+            t = t_of[i]
+            for a in tiles:
                 nc.vector.scalar_tensor_tensor(
                     out=t[:, a, :],
                     in0=y_of[i][:, a, :],
@@ -164,44 +171,41 @@ def tile_selfattention_pa_t_kernel(tc, h_attn, x, out_w_words, out_w_scales, ln_
                     op0=ALU.add,
                     op1=ALU.mult,
                 )
-            t_of[i] = t
 
-        def scale_offset_store(i):
-            t, rstd = t_of[i], rstd_of[i]
-            last = QUAD - 1
-            kept = E - VECTOR_SHARE
+        def scale(i, a, width=E):
+            t = t_of[i]
+            nc.scalar.activation(out=t[:, a, 0:width], in_=t[:, a, 0:width], func=ACT.Copy, scale=rstd_of[i][:, a : a + 1])
+
+        def offset(i, first, width):
+            some = t_of[i][:].rearrange("p a e -> p (a e)")[:, first * E : first * E + width]
+            nc.gpsimd.tensor_tensor(out=some, in0=some, in1=beta_twice[:, 0:width], op=ALU.add)
+
+        def finish(i, a, start=0):
+            t = t_of[i]
             nc.vector.scalar_tensor_tensor(
-                out=t[:, last, kept:E],
-                in0=t[:, last, kept:E],
-                scalar=rstd[:, last : last + 1],
-                in1=beta_bank[:, kept:E],
+                out=t[:, a, start:E],
+                in0=t[:, a, start:E],
+                scalar=rstd_of[i][:, a : a + 1],
+                in1=beta_bank[:, start:E],
                 op0=ALU.mult,
                 op1=ALU.add,
             )
-            for a in range(last):
-                nc.scalar.activation(out=t[:, a, :], in_=t[:, a, :], func=ACT.Copy, scale=rstd[:, a : a + 1])
-            nc.scalar.activation(out=t[:, last, 0:kept], in_=t[:, last, 0:kept], func=ACT.Copy, scale=rstd[:, last : last + 1])
-            for a in range(PAIR):
-                nc.gpsimd.tensor_tensor(out=t[:, a, :], in0=t[:, a, :], in1=beta_twice[:, 0:E], op=ALU.add)
-            nc.sync.dma_start(out=token_rows(out, i)[:, 0:PAIR, :], in_=t[:, 0:PAIR, :])
-            rest = t[:, PAIR:QUAD, :].rearrange("p a e -> p (a e)")[:, 0 : E + kept]
-            nc.gpsimd.tensor_tensor(out=rest, in0=rest, in1=beta_twice[:, 0 : E + kept], op=ALU.add)
-            nc.sync.dma_start(out=token_rows(out, i)[:, PAIR:QUAD, :], in_=t[:, PAIR:QUAD, :])
 
-        def finish_on_vector(i):
-            t, rstd = t_of[i], rstd_of[i]
-            for pair in range(QUAD // PAIR):
-                both = slice(pair * PAIR, (pair + 1) * PAIR)
-                for a in range(pair * PAIR, (pair + 1) * PAIR):
-                    nc.vector.scalar_tensor_tensor(
-                        out=t[:, a, :],
-                        in0=t[:, a, :],
-                        scalar=rstd[:, a : a + 1],
-                        in1=beta_bank[:],
-                        op0=ALU.mult,
-                        op1=ALU.add,
-                    )
-                nc.sync.dma_start(out=token_rows(out, i)[:, both, :], in_=t[:, both, :])
+        def store(i, tiles):
+            nc.sync.dma_start(out=token_rows(out, i)[:, tiles, :], in_=t_of[i][:, tiles, :])
+
+        def scale_offset_store(i):
+            last = QUAD - 1
+            kept = E - VECTOR_SHARE
+            finish(i, last, kept)
+            for a in range(last):
+                scale(i, a)
+            scale(i, last, kept)
+            for a in range(PAIR):
+                offset(i, a, E)
+            store(i, slice(0, PAIR))
+            offset(i, PAIR, E + kept)
+            store(i, slice(PAIR, QUAD))
 
         def step(n):
             if n >= 0 and live(n + HEADS_AHEAD):
@@ -216,10 +220,8 @@ def tile_selfattention_pa_t_kernel(tc, h_attn, x, out_w_words, out_w_scales, ln_
                 project(n + 1)
             if live(n + 3):
                 flip(n + 3)
-            if live(n - 1) and n - 1 < N_QUADS - VECTOR_TAIL:
+            if live(n - 1):
                 scale_offset_store(n - 1)
-            if live(n - 1) and n - 1 >= N_QUADS - VECTOR_TAIL:
-                finish_on_vector(n - 1)
             if live(n):
                 centre_and_gain(n)
                 deviation(n)
@@ -267,5 +269,31 @@ def tile_selfattention_pa_t_kernel(tc, h_attn, x, out_w_words, out_w_scales, ln_
         for a in range(PAIR):
             nc.scalar.copy(out=beta_twice[:, a * E : (a + 1) * E], in_=beta_bank[:])
 
-        for n in range(0, N_QUADS + 2):
+        for n in range(0, N_QUADS - 1):
             step(n)
+
+        before, final = N_QUADS - 2, N_QUADS - 1
+        early = QUAD - 1
+        for a in range(PAIR):
+            scale(before, a)
+            offset(before, a, E)
+        add_residual(final)
+        negate_mean(final)
+        deviation(final, slice(early, QUAD))
+        finish(before, PAIR)
+        centre_and_gain(final, (early,))
+        finish(before, PAIR + 1)
+        store(before, slice(PAIR, QUAD))
+        store(before, slice(0, PAIR))
+        squares_of(final, 0)
+        scale(final, early)
+        offset(final, early, E)
+        store(final, slice(early, QUAD))
+        squares_of(final, 1)
+        squares_of(final, 2)
+        inverse_deviation(final, slice(0, early))
+        centre_and_gain(final, (0, 1, 2))
+        for a in range(early):
+            finish(final, a)
+        store(final, slice(0, PAIR))
+        store(final, slice(PAIR, early))

@@ -195,16 +195,15 @@ def tile_selfattention_pa_t_kernel(tc, h_attn, x, out_w_words, out_w_scales, ln_
             nc.sync.dma_start(out=token_rows(out, i)[:, tiles, :], in_=t_of[i][:, tiles, :])
 
         def scale_offset_store(i):
-            last = QUAD - 1
             kept = E - VECTOR_SHARE
-            finish(i, last, kept)
-            for a in range(last):
+            finish(i, 0, kept)
+            scale(i, 0, kept)
+            for a in range(1, QUAD):
                 scale(i, a)
-            scale(i, last, kept)
-            for a in range(PAIR):
-                offset(i, a, E)
+            offset(i, 0, kept)
+            offset(i, 1, E)
             store(i, slice(0, PAIR))
-            offset(i, PAIR, E + kept)
+            offset(i, PAIR, PAIR * E)
             store(i, slice(PAIR, QUAD))
 
         def step(n):

@@ -23,6 +23,7 @@ QUAD = 4
 QUAD_TOKENS = P * QUAD
 N_QUADS = B * S // QUAD_TOKENS
 PAIR = 2
+BOTH_PAIRS = (0, 1)
 HEADS_AHEAD = 7
 RESID_AHEAD = 4
 VECTOR_SHARE = E // 2
@@ -81,15 +82,15 @@ def tile_selfattention_pa_t_kernel(tc, h_attn, x, out_w_words, out_w_scales, ln_
                         nc.tensor.transpose(flipped[:, a, u, :], words[:, pair * PAIR + a, u : E // 2 : 2], ident[:])
                 flipped_of[i].append(flipped)
 
-        def regroup(i):
-            grouped = grouped_rows.tile([P, QUAD, P, PACK], BF16, align_bytes=64, name="grouped")
-            grouped_words = grouped[:].bitcast(F32)
-            for pair in range(QUAD // PAIR):
+        def regroup(i, pairs):
+            if i not in grouped_of:
+                grouped_of[i] = grouped_rows.tile([P, QUAD, P, PACK], BF16, align_bytes=64, name="grouped")
+            grouped_words = grouped_of[i][:].bitcast(F32)
+            for pair in pairs:
                 nc.scalar.copy(
                     out=grouped_words[:, pair * PAIR : (pair + 1) * PAIR, :, :],
                     in_=flipped_of[i][pair][:].rearrange("p a u n -> p a n u"),
                 )
-            grouped_of[i] = grouped
 
         def quantise(i):
             codes = work.tile([P, QUAD * P], U32, align_bytes=64, name="codes")
@@ -153,11 +154,6 @@ def tile_selfattention_pa_t_kernel(tc, h_attn, x, out_w_words, out_w_scales, ln_
                 out=rstd_of[i][:, tiles], in_=sum_sq_of[i][:, tiles], func=ACT.Abs_reciprocal_sqrt, bias=eps[:], scale=1.0 / E
             )
 
-        def deviation(i, tiles=slice(0, QUAD)):
-            for a in range(tiles.start, tiles.stop):
-                squares_of(i, a)
-            inverse_deviation(i, tiles)
-
         def centre_and_gain(i, tiles=(0, 1, 2, 3)):
             if i not in t_of:
                 t_of[i] = out_rows.tile([P, QUAD, E], F32, name="t")
@@ -176,9 +172,13 @@ def tile_selfattention_pa_t_kernel(tc, h_attn, x, out_w_words, out_w_scales, ln_
             t = t_of[i]
             nc.scalar.activation(out=t[:, a, 0:width], in_=t[:, a, 0:width], func=ACT.Copy, scale=rstd_of[i][:, a : a + 1])
 
-        def offset(i, first, width):
-            some = t_of[i][:].rearrange("p a e -> p (a e)")[:, first * E : first * E + width]
-            nc.gpsimd.tensor_tensor(out=some, in0=some, in1=beta_twice[:, 0:width], op=ALU.add)
+        def offset(i, a, width=E):
+            some = t_of[i][:, a, 0:width]
+            nc.gpsimd.tensor_tensor(out=some, in0=some, in1=beta_all[:, 0:width], op=ALU.add)
+
+        def offset_pair(i, tiles):
+            both = t_of[i][:, tiles, :]
+            nc.gpsimd.tensor_tensor(out=both, in0=both, in1=beta_all[:].unsqueeze(1).to_broadcast([P, PAIR, E]), op=ALU.add)
 
         def finish(i, a, start=0):
             t = t_of[i]
@@ -201,31 +201,34 @@ def tile_selfattention_pa_t_kernel(tc, h_attn, x, out_w_words, out_w_scales, ln_
             for a in range(1, QUAD):
                 scale(i, a)
             offset(i, 0, kept)
-            offset(i, 1, E)
+            offset(i, 1)
             store(i, slice(0, PAIR))
-            offset(i, PAIR, PAIR * E)
+            offset_pair(i, slice(PAIR, QUAD))
             store(i, slice(PAIR, QUAD))
 
-        def step(n):
-            if n >= 0 and live(n + HEADS_AHEAD):
+        def ask_ahead(n):
+            if live(n + HEADS_AHEAD):
                 load_heads(n + HEADS_AHEAD)
-            if n >= 0 and live(n + RESID_AHEAD):
+            if live(n + RESID_AHEAD):
                 load_resid(n + RESID_AHEAD)
-            if live(n):
-                add_residual(n)
-                negate_mean(n)
-            if live(n + 1):
-                quantise(n + 1)
-                project(n + 1)
+
+        def step(n):
+            ask_ahead(n)
+            add_residual(n)
+            negate_mean(n)
+            quantise(n + 1)
+            project(n + 1)
             if live(n + 3):
                 flip(n + 3)
-            if live(n - 1):
-                scale_offset_store(n - 1)
-            if live(n):
-                centre_and_gain(n)
-                deviation(n)
+            scale_offset_store(n - 1)
+            centre_and_gain(n)
+            for a in range(QUAD):
+                squares_of(n, a)
             if live(n + 3):
-                regroup(n + 3)
+                regroup(n + 3, (0,))
+            inverse_deviation(n, slice(0, QUAD))
+            if live(n + 3):
+                regroup(n + 3, (1,))
 
         w_plane = keep.tile([P, E], U8, align_bytes=64)
         nc.vector.memset(w_plane[:].bitcast(I32), 0)
@@ -248,8 +251,8 @@ def tile_selfattention_pa_t_kernel(tc, h_attn, x, out_w_words, out_w_scales, ln_
                 out=w_plane[32 * quadrant : 32 * quadrant + 4, :].bitcast(I32),
                 in_=out_w_scales[0, 4 * quadrant : 4 * quadrant + 4, :].bitcast(I32),
             )
-        load_heads(1)
         load_resid(0)
+        load_heads(1)
         nc.sync.dma_start(out=gain_rows[0:1, 0, :], in_=ln_gamma.unsqueeze(0))
         nc.sync.dma_start(out=gain_rows[0:1, 1, :], in_=ln_beta.unsqueeze(0))
         for i in range(2, HEADS_AHEAD):
@@ -257,38 +260,56 @@ def tile_selfattention_pa_t_kernel(tc, h_attn, x, out_w_words, out_w_scales, ln_
             if i - 1 < RESID_AHEAD:
                 load_resid(i - 1)
 
-        for n in range(-3, 0):
-            step(n)
-
+        flip(0)
+        regroup(0, BOTH_PAIRS)
+        quantise(0)
+        project(0)
+        flip(1)
+        regroup(1, BOTH_PAIRS)
         gamma_all = gain_banks.tile([P, E], F32)
         nc.tensor.matmul(out=gamma_all[:], lhsT=ones[:], rhs=gain_rows[:, 0, :], start=True, stop=True)
         beta_bank = gain_banks.tile([P, E], F32)
         nc.tensor.matmul(out=beta_bank[:], lhsT=ones[:], rhs=gain_rows[:, 1, :], start=True, stop=True)
-        beta_twice = keep.tile([P, PAIR * E], F32)
-        for a in range(PAIR):
-            nc.scalar.copy(out=beta_twice[:, a * E : (a + 1) * E], in_=beta_bank[:])
 
-        for n in range(0, N_QUADS - 1):
+        ask_ahead(0)
+        add_residual(0)
+        negate_mean(0)
+        quantise(1)
+        project(1)
+        flip(2)
+        centre_and_gain(0)
+        for a in range(QUAD):
+            squares_of(0, a)
+        regroup(2, (0,))
+        inverse_deviation(0, slice(0, QUAD))
+        regroup(2, (1,))
+        beta_all = keep.tile([P, E], F32)
+        nc.scalar.copy(out=beta_all[:], in_=beta_bank[:])
+        flip(3)
+        regroup(3, BOTH_PAIRS)
+
+        for n in range(1, N_QUADS - 1):
             step(n)
 
         before, final = N_QUADS - 2, N_QUADS - 1
         early = QUAD - 1
         for a in range(PAIR):
             scale(before, a)
-            offset(before, a, E)
+            offset(before, a)
         add_residual(final)
         negate_mean(final)
-        deviation(final, slice(early, QUAD))
+        squares_of(final, early)
+        squares_of(final, 0)
+        inverse_deviation(final, slice(early, QUAD))
         finish(before, PAIR)
         centre_and_gain(final, (early,))
         finish(before, PAIR + 1)
         store(before, slice(PAIR, QUAD))
         store(before, slice(0, PAIR))
-        squares_of(final, 0)
-        scale(final, early)
-        offset(final, early, E)
-        store(final, slice(early, QUAD))
         squares_of(final, 1)
+        scale(final, early)
+        offset(final, early)
+        store(final, slice(early, QUAD))
         squares_of(final, 2)
         inverse_deviation(final, slice(0, early))
         centre_and_gain(final, (0, 1, 2))

@@ -41,7 +41,7 @@ def tile_selfattention_pa_t_kernel(tc, h_attn, x, out_w_words, out_w_scales, ln_
         work = ctx.enter_context(tc.tile_pool(name="work", bufs=2))
         grouped_rows = ctx.enter_context(tc.tile_pool(name="grouped_rows", bufs=3))
         sums_rows = ctx.enter_context(tc.tile_pool(name="sums_rows", bufs=3))
-        out_rows = ctx.enter_context(tc.tile_pool(name="out_rows", bufs=4))
+        out_rows = ctx.enter_context(tc.tile_pool(name="out_rows", bufs=8))
         stats = ctx.enter_context(tc.tile_pool(name="stats", bufs=4))
         gain_banks = ctx.enter_context(tc.psum_pool(name="gain_banks", bufs=1))
         flip_banks = ctx.enter_context(tc.psum_pool(name="flip_banks", bufs=2))

@@ -24,9 +24,12 @@ QUAD_TOKENS = P * QUAD
 N_QUADS = B * S // QUAD_TOKENS
 PAIR = 2
 BOTH_PAIRS = (0, 1)
-HEADS_AHEAD = 7
+N_TILES = N_QUADS * QUAD
+COLUMN = {3: 0, 2: 1, 0: 2, 1: 3}
+HEADS_AHEAD = 6
 RESID_AHEAD = 4
-VECTOR_SHARE = E // 2
+KEPT = E - 32
+EARLY = E - 128
 
 FLOPS = 2 * B * S * E * E
 
@@ -42,13 +45,13 @@ def tile_selfattention_pa_t_kernel(tc, h_attn, x, out_w_words, out_w_scales, ln_
         grouped_rows = ctx.enter_context(tc.tile_pool(name="grouped_rows", bufs=3))
         sums_rows = ctx.enter_context(tc.tile_pool(name="sums_rows", bufs=3))
         out_rows = ctx.enter_context(tc.tile_pool(name="out_rows", bufs=8))
-        stats = ctx.enter_context(tc.tile_pool(name="stats", bufs=4))
+        stats = ctx.enter_context(tc.tile_pool(name="stats", bufs=5))
         gain_banks = ctx.enter_context(tc.psum_pool(name="gain_banks", bufs=1))
         flip_banks = ctx.enter_context(tc.psum_pool(name="flip_banks", bufs=2))
         acc_banks = ctx.enter_context(tc.psum_pool(name="acc_banks", bufs=4))
 
         merged_of, resid_of, flipped_of, grouped_of, codes_of, plane_of = {}, {}, {}, {}, {}, {}
-        acc_of, y_of, sums_of, neg_mean_of, sum_sq_of, rstd_of, t_of = {}, {}, {}, {}, {}, {}, {}
+        acc_of, y_of, t_of, stats_of = {}, {}, {}, {}
 
         def live(i):
             return 0 <= i < N_QUADS
@@ -67,15 +70,16 @@ def tile_selfattention_pa_t_kernel(tc, h_attn, x, out_w_words, out_w_scales, ln_
                 )
             merged_of[i] = merged
 
-        def load_resid(i):
-            resid = resid_in.tile([P, QUAD, E], BF16, name="resid")
-            nc.sync.dma_start(out=resid[:], in_=token_rows(x, i))
-            resid_of[i] = resid
+        def load_resid(i, parts=(slice(0, QUAD),)):
+            if i not in resid_of:
+                resid_of[i] = resid_in.tile([P, QUAD, E], BF16, name="resid")
+            for tiles in parts:
+                nc.sync.dma_start(out=resid_of[i][:, tiles, :], in_=token_rows(x, i)[:, tiles, :])
 
-        def flip(i):
+        def flip(i, pairs=BOTH_PAIRS):
             words = merged_of[i][:].bitcast(F32)
-            flipped_of[i] = []
-            for pair in range(QUAD // PAIR):
+            flipped_of.setdefault(i, [])
+            for pair in pairs:
                 flipped = flip_banks.tile([P, PAIR, 2, P], F32, name="flipped")
                 for a in range(PAIR):
                     for u in range(2):
@@ -92,19 +96,20 @@ def tile_selfattention_pa_t_kernel(tc, h_attn, x, out_w_words, out_w_scales, ln_
                     in_=flipped_of[i][pair][:].rearrange("p a u n -> p a n u"),
                 )
 
-        def quantise(i):
-            codes = work.tile([P, QUAD * P], U32, align_bytes=64, name="codes")
-            plane = work.tile([P, QUAD * P], U8, align_bytes=64, name="plane")
+        def quantise(i, tiles=slice(0, QUAD)):
+            if i not in codes_of:
+                codes_of[i] = work.tile([P, QUAD * P], U32, align_bytes=64, name="codes")
+                plane_of[i] = work.tile([P, QUAD * P], U8, align_bytes=64, name="plane")
+            columns = slice(tiles.start * P, tiles.stop * P)
             nc.vector.quantize_mx(
-                out=codes[:].bitcast(FP8X4),
-                scales=plane[:],
-                in_=grouped_of[i][:].rearrange("p a n t -> p (a n t)"),
+                out=codes_of[i][:, columns].bitcast(FP8X4),
+                scales=plane_of[i][:, columns],
+                in_=grouped_of[i][:, tiles, :, :].rearrange("p a n t -> p (a n t)"),
             )
-            codes_of[i], plane_of[i] = codes, plane
 
-        def project(i):
-            acc_of[i] = []
-            for a in range(QUAD):
+        def project(i, tiles=(0, 1, 2, 3)):
+            acc_of.setdefault(i, [])
+            for a in tiles:
                 acc = acc_banks.tile([P, E], F32, name="acc")
                 nc.tensor.matmul_mx(
                     out=acc[:],
@@ -117,94 +122,105 @@ def tile_selfattention_pa_t_kernel(tc, h_attn, x, out_w_words, out_w_scales, ln_
                 )
                 acc_of[i].append(acc)
 
-        def add_residual(i):
-            y = sums_rows.tile([P, QUAD, E], F32, name="y")
-            sums = stats.tile([P, QUAD], F32, name="sums")
-            neg_mean_of[i] = stats.tile([P, QUAD], F32, name="neg_mean")
-            sum_sq_of[i] = stats.tile([P, QUAD], F32, name="sum_sq")
-            rstd_of[i] = stats.tile([P, QUAD], F32, name="rstd")
-            for a in range(QUAD):
+        def group_tiles(g):
+            return [j for j in range(g * QUAD - 1, (g + 1) * QUAD - 1) if 0 <= j < N_TILES]
+
+        def stats_tile(kind, j):
+            g = (j + 1) // QUAD
+            if (kind, g) not in stats_of:
+                stats_of[kind, g] = stats.tile([P, QUAD], F32, name=kind)
+            return stats_of[kind, g]
+
+        def stat(kind, j):
+            column = COLUMN[j % QUAD]
+            return stats_tile(kind, j)[:, column : column + 1]
+
+        def some_stats(kind, tiles):
+            columns = sorted(COLUMN[j % QUAD] for j in tiles)
+            return stats_tile(kind, tiles[0])[:, columns[0] : columns[-1] + 1]
+
+        def rows(store_of, pool, name, j):
+            if j // QUAD not in store_of:
+                store_of[j // QUAD] = pool.tile([P, QUAD, E], F32, name=name)
+            return store_of[j // QUAD][:, j % QUAD, :]
+
+        def y_at(j):
+            return rows(y_of, sums_rows, "y", j)
+
+        def t_at(j):
+            return rows(t_of, out_rows, "t", j)
+
+        def add_residual(tiles):
+            for j in tiles:
                 nc.vector.scalar_tensor_tensor(
-                    out=y[:, a, :],
-                    in0=acc_of[i][a][:],
+                    out=y_at(j),
+                    in0=acc_of[j // QUAD][j % QUAD][:],
                     scalar=1.0,
-                    in1=resid_of[i][:, a, :],
+                    in1=resid_of[j // QUAD][:, j % QUAD, :],
                     op0=ALU.mult,
                     op1=ALU.add,
-                    accum_out=sums[:, a : a + 1],
+                    accum_out=stat("sums", j),
                 )
-            y_of[i], sums_of[i] = y, sums
 
-        def negate_mean(i, tiles=slice(0, QUAD)):
-            nc.scalar.activation(out=neg_mean_of[i][:, tiles], in_=sums_of[i][:, tiles], func=ACT.Copy, scale=-1.0 / E)
+        def negate_mean(tiles):
+            nc.scalar.activation(
+                out=some_stats("neg_mean", tiles), in_=some_stats("sums", tiles), func=ACT.Copy, scale=-1.0 / E
+            )
 
-        def squares_of(i, a):
+        def squares_of(j):
             squares = work.tile([P, E], BF16, name="squares")
             nc.scalar.activation(
-                out=squares[:],
-                in_=y_of[i][:, a, :],
-                func=ACT.Square,
-                bias=neg_mean_of[i][:, a : a + 1],
-                scale=1.0,
-                accum_out=sum_sq_of[i][:, a : a + 1],
+                out=squares[:], in_=y_at(j), func=ACT.Square, bias=stat("neg_mean", j), scale=1.0, accum_out=stat("sum_sq", j)
             )
 
-        def inverse_deviation(i, tiles):
+        def inverse_deviation(tiles):
             nc.scalar.activation(
-                out=rstd_of[i][:, tiles], in_=sum_sq_of[i][:, tiles], func=ACT.Abs_reciprocal_sqrt, bias=eps[:], scale=1.0 / E
+                out=some_stats("rstd", tiles),
+                in_=some_stats("sum_sq", tiles),
+                func=ACT.Abs_reciprocal_sqrt,
+                bias=eps[:],
+                scale=1.0 / E,
             )
 
-        def centre_and_gain(i, tiles=(0, 1, 2, 3)):
-            if i not in t_of:
-                t_of[i] = out_rows.tile([P, QUAD, E], F32, name="t")
-            t = t_of[i]
-            for a in tiles:
-                nc.vector.scalar_tensor_tensor(
-                    out=t[:, a, :],
-                    in0=y_of[i][:, a, :],
-                    scalar=neg_mean_of[i][:, a : a + 1],
-                    in1=gamma_all[:],
-                    op0=ALU.add,
-                    op1=ALU.mult,
-                )
+        def shift_of(j):
+            nc.scalar.activation(out=stat("shift", j), in_=stat("neg_mean", j), func=ACT.Copy, scale=stat("rstd", j))
 
-        def scale(i, a, width=E):
-            t = t_of[i]
-            nc.scalar.activation(out=t[:, a, 0:width], in_=t[:, a, 0:width], func=ACT.Copy, scale=rstd_of[i][:, a : a + 1])
+        def standardise(j, start=0, stop=E):
+            nc.scalar.activation(
+                out=t_at(j)[:, start:stop], in_=y_at(j)[:, start:stop], func=ACT.Identity, bias=stat("shift", j), scale=stat("rstd", j)
+            )
 
-        def offset(i, a, width=E):
-            some = t_of[i][:, a, 0:width]
-            nc.gpsimd.tensor_tensor(out=some, in0=some, in1=beta_all[:, 0:width], op=ALU.add)
-
-        def offset_pair(i, tiles):
-            both = t_of[i][:, tiles, :]
-            nc.gpsimd.tensor_tensor(out=both, in0=both, in1=beta_all[:].unsqueeze(1).to_broadcast([P, PAIR, E]), op=ALU.add)
-
-        def finish(i, a, start=0):
-            t = t_of[i]
+        def centre_and_gain(j):
             nc.vector.scalar_tensor_tensor(
-                out=t[:, a, start:E],
-                in0=t[:, a, start:E],
-                scalar=rstd_of[i][:, a : a + 1],
-                in1=beta_bank[:, start:E],
-                op0=ALU.mult,
-                op1=ALU.add,
+                out=t_at(j), in0=y_at(j), scalar=stat("neg_mean", j), in1=gamma_all[:], op0=ALU.add, op1=ALU.mult
             )
 
-        def store(i, tiles):
-            nc.sync.dma_start(out=token_rows(out, i)[:, tiles, :], in_=t_of[i][:, tiles, :])
+        def finish(j):
+            nc.vector.scalar_tensor_tensor(
+                out=t_at(j), in0=t_at(j), scalar=stat("rstd", j), in1=beta_bank[:], op0=ALU.mult, op1=ALU.add
+            )
 
-        def scale_offset_store(i):
-            kept = E - VECTOR_SHARE
-            finish(i, 0, kept)
-            scale(i, 0, kept)
-            for a in range(1, QUAD):
-                scale(i, a)
-            offset(i, 0, kept)
-            offset(i, 1)
-            store(i, slice(0, PAIR))
-            offset_pair(i, slice(PAIR, QUAD))
-            store(i, slice(PAIR, QUAD))
+        def scale(j):
+            nc.scalar.activation(out=t_at(j), in_=t_at(j), func=ACT.Copy, scale=stat("rstd", j))
+
+        def wide(row, count):
+            return row.unsqueeze(1).to_broadcast([P, count, row.shape[-1]])
+
+        def gain(i, tiles=slice(0, PAIR)):
+            some = t_of[i][:, tiles, :]
+            nc.gpsimd.tensor_tensor(out=some, in0=some, in1=wide(gamma_row[:], tiles.stop - tiles.start), op=ALU.mult)
+
+        def offset(i, tiles=slice(0, PAIR), width=KEPT):
+            some = t_of[i][:, tiles, 0:width]
+            nc.gpsimd.tensor_tensor(out=some, in0=some, in1=wide(beta_row[:, 0:width], tiles.stop - tiles.start), op=ALU.add)
+
+        def offset_rest(i):
+            some = t_of[i][:, 0:PAIR, KEPT:E]
+            nc.vector.tensor_tensor(out=some, in0=some, in1=wide(beta_bank[:, KEPT:E], PAIR), op=ALU.add)
+
+        def store(j, count=PAIR):
+            tiles = slice(j % QUAD, j % QUAD + count)
+            nc.sync.dma_start(out=token_rows(out, j // QUAD)[:, tiles, :], in_=t_of[j // QUAD][:, tiles, :])
 
         def ask_ahead(n):
             if live(n + HEADS_AHEAD):
@@ -212,23 +228,53 @@ def tile_selfattention_pa_t_kernel(tc, h_attn, x, out_w_words, out_w_scales, ln_
             if live(n + RESID_AHEAD):
                 load_resid(n + RESID_AHEAD)
 
+        def quad_tiles(n):
+            return range(n * QUAD, (n + 1) * QUAD)
+
+        def vector_tiles(g):
+            return [j for j in group_tiles(g) if j % QUAD >= PAIR]
+
+        def pair_of(n):
+            return [n * QUAD, n * QUAD + 1]
+
         def step(n):
+            group, pair = group_tiles(n), pair_of(n)
             ask_ahead(n)
-            add_residual(n)
-            negate_mean(n)
+            add_residual(quad_tiles(n))
+            negate_mean(group)
             quantise(n + 1)
+            if live(n + 2):
+                flip(n + 2)
             project(n + 1)
-            if live(n + 3):
-                flip(n + 3)
-            scale_offset_store(n - 1)
-            centre_and_gain(n)
-            for a in range(QUAD):
-                squares_of(n, a)
-            if live(n + 3):
-                regroup(n + 3, (0,))
-            inverse_deviation(n, slice(0, QUAD))
-            if live(n + 3):
-                regroup(n + 3, (1,))
+            if n > 0:
+                standardise(pair_of(n - 1)[1], EARLY)
+                gain(n - 1)
+                offset(n - 1)
+            if n > 1:
+                offset_rest(n - 2)
+                store(pair_of(n - 2)[0])
+            for j in vector_tiles(n - 1):
+                finish(j)
+                if j % QUAD == QUAD - 1:
+                    store(j - 1)
+            for j in vector_tiles(n):
+                centre_and_gain(j)
+            for j in pair:
+                squares_of(j)
+            if live(n + 2):
+                regroup(n + 2, (0,))
+            inverse_deviation(pair)
+            v = vector_tiles(n)
+            squares_of(v[0])
+            for j in pair:
+                shift_of(j)
+            if len(v) > 1:
+                squares_of(v[1])
+            standardise(pair[0])
+            standardise(pair[1], 0, EARLY)
+            if live(n + 2):
+                regroup(n + 2, (1,))
+            inverse_deviation(v)
 
         w_plane = keep.tile([P, E], U8, align_bytes=64)
         nc.vector.memset(w_plane[:].bitcast(I32), 0)
@@ -270,50 +316,53 @@ def tile_selfattention_pa_t_kernel(tc, h_attn, x, out_w_words, out_w_scales, ln_
         nc.tensor.matmul(out=gamma_all[:], lhsT=ones[:], rhs=gain_rows[:, 0, :], start=True, stop=True)
         beta_bank = gain_banks.tile([P, E], F32)
         nc.tensor.matmul(out=beta_bank[:], lhsT=ones[:], rhs=gain_rows[:, 1, :], start=True, stop=True)
+        gamma_row = keep.tile([P, E], F32)
+        beta_row = keep.tile([P, E], F32)
 
-        ask_ahead(0)
-        add_residual(0)
-        negate_mean(0)
-        quantise(1)
-        project(1)
-        flip(2)
-        centre_and_gain(0)
-        for a in range(QUAD):
-            squares_of(0, a)
-        regroup(2, (0,))
-        inverse_deviation(0, slice(0, QUAD))
-        regroup(2, (1,))
-        beta_all = keep.tile([P, E], F32)
-        nc.scalar.copy(out=beta_all[:], in_=beta_bank[:])
-        flip(3)
-        regroup(3, BOTH_PAIRS)
-
+        step(0)
+        nc.scalar.copy(out=gamma_row[:], in_=gamma_all[:])
+        nc.scalar.copy(out=beta_row[:], in_=beta_bank[:])
         for n in range(1, N_QUADS - 1):
             step(n)
 
-        before, final = N_QUADS - 2, N_QUADS - 1
-        early = QUAD - 1
-        for a in range(PAIR):
-            scale(before, a)
-            offset(before, a)
-        add_residual(final)
-        negate_mean(final)
-        squares_of(final, early)
-        squares_of(final, 0)
-        inverse_deviation(final, slice(early, QUAD))
-        finish(before, PAIR)
-        centre_and_gain(final, (early,))
-        finish(before, PAIR + 1)
-        store(before, slice(PAIR, QUAD))
-        store(before, slice(0, PAIR))
-        squares_of(final, 1)
-        scale(final, early)
-        offset(final, early)
-        store(final, slice(early, QUAD))
-        squares_of(final, 2)
-        inverse_deviation(final, slice(0, early))
-        centre_and_gain(final, (0, 1, 2))
-        for a in range(early):
-            finish(final, a)
-        store(final, slice(0, PAIR))
-        store(final, slice(PAIR, early))
+        n = N_QUADS - 1
+        group, pair = group_tiles(n), pair_of(n)
+        end = N_TILES - 1
+        add_residual(quad_tiles(n))
+        negate_mean(group)
+        standardise(pair_of(n - 1)[1], EARLY)
+        gain(n - 1)
+        offset(n - 1)
+        offset_rest(n - 2)
+        store(pair_of(n - 2)[0])
+        for j in vector_tiles(n - 1):
+            finish(j)
+            if j % QUAD == QUAD - 1:
+                store(j - 1)
+        squares_of(group[0])
+        squares_of(pair[0])
+        inverse_deviation(group[0:1])
+        squares_of(pair[1])
+        inverse_deviation(pair)
+        negate_mean([end])
+        squares_of(pair[1] + 1)
+        centre_and_gain(group[0])
+        centre_and_gain(pair[0])
+        scale(pair[0])
+        offset(n, slice(0, 1), E)
+        finish(group[0])
+        store(group[0] - 1)
+        centre_and_gain(pair[1])
+        offset_rest(n - 1)
+        store(pair_of(n - 1)[0])
+        centre_and_gain(pair[1] + 1)
+        squares_of(end)
+        inverse_deviation([pair[1] + 1])
+        centre_and_gain(end)
+        inverse_deviation([end])
+        finish(pair[1])
+        store(pair[0])
+        finish(pair[1] + 1)
+        store(pair[1] + 1, 1)
+        finish(end)
+        store(end, 1)

@@ -70,6 +70,14 @@ def tile_selfattention_pa_t_kernel(tc, h_attn, x, out_w_words, out_w_scales, ln_
                 )
             merged_of[i] = merged
 
+        def load_heads_by_tile(i):
+            b, s0 = divmod(i * QUAD_TOKENS, S)
+            merged = heads_in.tile([P, QUAD, E], BF16, name="merged")
+            tokens = h_attn[b, :, s0 : s0 + QUAD_TOKENS, :].rearrange("h (p a) d -> p a h d", a=QUAD)
+            for a in range(QUAD):
+                nc.sync.dma_start(out=merged[:, a, :].rearrange("p (h d) -> p h d", h=H), in_=tokens[:, a, :, :])
+            merged_of[i] = merged
+
         def load_resid(i, parts=(slice(0, QUAD),)):
             if i not in resid_of:
                 resid_of[i] = resid_in.tile([P, QUAD, E], BF16, name="resid")
@@ -289,27 +297,39 @@ def tile_selfattention_pa_t_kernel(tc, h_attn, x, out_w_words, out_w_scales, ln_
         warm = keep.tile([P, 1], F32)
         nc.scalar.activation(out=warm[:], in_=eps[:], func=ACT.Abs_reciprocal_sqrt)
 
-        load_heads(0)
         w_words = keep.tile([P, 2 * E], U8, align_bytes=64)
-        nc.sync.dma_start(out=w_words[:].bitcast(I32), in_=out_w_words[0].bitcast(I32))
-        for quadrant in range(4):
+
+        def load_weight_scales(quadrant):
             nc.sync.dma_start(
                 out=w_plane[32 * quadrant : 32 * quadrant + 4, :].bitcast(I32),
                 in_=out_w_scales[0, 4 * quadrant : 4 * quadrant + 4, :].bitcast(I32),
             )
-        load_resid(0)
+
+        load_heads_by_tile(0)
+        nc.sync.dma_start(out=w_words[:].bitcast(I32), in_=out_w_words[0].bitcast(I32))
+        load_weight_scales(0)
+        load_weight_scales(1)
+        load_resid(0, (slice(0, PAIR),))
+        load_weight_scales(2)
+        load_weight_scales(3)
         load_heads(1)
+        load_resid(0, (slice(PAIR, QUAD),))
         nc.sync.dma_start(out=gain_rows[0:1, 0, :], in_=ln_gamma.unsqueeze(0))
         nc.sync.dma_start(out=gain_rows[0:1, 1, :], in_=ln_beta.unsqueeze(0))
-        for i in range(2, HEADS_AHEAD):
-            load_heads(i)
-            if i - 1 < RESID_AHEAD:
-                load_resid(i - 1)
+        load_heads(2)
+        load_resid(1)
+        load_heads(3)
+        load_resid(2)
+        load_heads(4)
+        load_resid(3)
+        load_heads(5)
 
-        flip(0)
-        regroup(0, BOTH_PAIRS)
-        quantise(0)
-        project(0)
+        for half in BOTH_PAIRS:
+            flip(0, (half,))
+            regroup(0, (half,))
+        for half in BOTH_PAIRS:
+            quantise(0, slice(half * PAIR, (half + 1) * PAIR))
+            project(0, (half * PAIR, half * PAIR + 1))
         flip(1)
         regroup(1, BOTH_PAIRS)
         gamma_all = gain_banks.tile([P, E], F32)
@@ -327,12 +347,13 @@ def tile_selfattention_pa_t_kernel(tc, h_attn, x, out_w_words, out_w_scales, ln_
 
         n = N_QUADS - 1
         group, pair = group_tiles(n), pair_of(n)
-        end = N_TILES - 1
+        third, end = pair[1] + 1, N_TILES - 1
+        standardise(pair_of(n - 1)[1], EARLY)
         add_residual(quad_tiles(n))
         negate_mean(group)
-        standardise(pair_of(n - 1)[1], EARLY)
         gain(n - 1)
-        offset(n - 1)
+        for a in range(PAIR):
+            offset(n - 1, slice(a, a + 1))
         offset_rest(n - 2)
         store(pair_of(n - 2)[0])
         for j in vector_tiles(n - 1):
@@ -345,24 +366,26 @@ def tile_selfattention_pa_t_kernel(tc, h_attn, x, out_w_words, out_w_scales, ln_
         squares_of(pair[1])
         inverse_deviation(pair)
         negate_mean([end])
-        squares_of(pair[1] + 1)
-        centre_and_gain(group[0])
         centre_and_gain(pair[0])
+        centre_and_gain(group[0])
+        centre_and_gain(pair[1])
+        squares_of(third)
         scale(pair[0])
+        squares_of(end)
+        inverse_deviation([third])
         offset(n, slice(0, 1), E)
         finish(group[0])
         store(group[0] - 1)
-        centre_and_gain(pair[1])
         offset_rest(n - 1)
-        store(pair_of(n - 1)[0])
-        centre_and_gain(pair[1] + 1)
-        squares_of(end)
-        inverse_deviation([pair[1] + 1])
-        centre_and_gain(end)
-        inverse_deviation([end])
+        store(pair_of(n - 1)[0], 1)
         finish(pair[1])
-        store(pair[0])
-        finish(pair[1] + 1)
-        store(pair[1] + 1, 1)
+        store(pair_of(n - 1)[1], 1)
+        store(pair[1], 1)
+        centre_and_gain(third)
+        inverse_deviation([end])
+        centre_and_gain(end)
+        finish(third)
+        store(third, 1)
         finish(end)
+        store(pair[0], 1)
         store(end, 1)

@@ -94,12 +94,12 @@ def tile_selfattention_pa_t_kernel(tc, h_attn, x, out_w_words, out_w_scales, ln_
                         nc.tensor.transpose(flipped[:, a, u, :], words[:, pair * PAIR + a, u : E // 2 : 2], ident[:])
                 flipped_of[i].append(flipped)
 
-        def regroup(i, pairs):
+        def regroup(i, pairs, copy=nc.scalar.copy):
             if i not in grouped_of:
                 grouped_of[i] = grouped_rows.tile([P, QUAD, P, PACK], BF16, align_bytes=64, name="grouped")
             grouped_words = grouped_of[i][:].bitcast(F32)
             for pair in pairs:
-                nc.scalar.copy(
+                copy(
                     out=grouped_words[:, pair * PAIR : (pair + 1) * PAIR, :, :],
                     in_=flipped_of[i][pair][:].rearrange("p a u n -> p a n u"),
                 )
@@ -116,7 +116,7 @@ def tile_selfattention_pa_t_kernel(tc, h_attn, x, out_w_words, out_w_scales, ln_
             )
 
         def project(i, tiles=(0, 1, 2, 3)):
-            acc_of.setdefault(i, [])
+            acc_of.setdefault(i, {})
             for a in tiles:
                 acc = acc_banks.tile([P, E], F32, name="acc")
                 nc.tensor.matmul_mx(
@@ -128,7 +128,7 @@ def tile_selfattention_pa_t_kernel(tc, h_attn, x, out_w_words, out_w_scales, ln_
                     start=True,
                     stop=True,
                 )
-                acc_of[i].append(acc)
+                acc_of[i][a] = acc
 
         def group_tiles(g):
             return [j for j in range(g * QUAD - 1, (g + 1) * QUAD - 1) if 0 <= j < N_TILES]
@@ -247,13 +247,14 @@ def tile_selfattention_pa_t_kernel(tc, h_attn, x, out_w_words, out_w_scales, ln_
 
         def step(n):
             group, pair = group_tiles(n), pair_of(n)
-            ask_ahead(n)
-            add_residual(quad_tiles(n))
+            if n > 0:
+                ask_ahead(n)
+                add_residual(quad_tiles(n))
             negate_mean(group)
             quantise(n + 1)
             if live(n + 2):
                 flip(n + 2)
-            project(n + 1)
+            project(n + 1, (1, 0, 3, 2) if n > 0 else (0, 1, 2, 3))
             if n > 0:
                 standardise(pair_of(n - 1)[1], EARLY)
                 gain(n - 1)
@@ -306,16 +307,16 @@ def tile_selfattention_pa_t_kernel(tc, h_attn, x, out_w_words, out_w_scales, ln_
             )
 
         load_heads_by_tile(0)
+        nc.sync.dma_start(out=gain_rows[0:1, 0, :], in_=ln_gamma.unsqueeze(0))
+        nc.sync.dma_start(out=gain_rows[0:1, 1, :], in_=ln_beta.unsqueeze(0))
         nc.sync.dma_start(out=w_words[:].bitcast(I32), in_=out_w_words[0].bitcast(I32))
         load_weight_scales(0)
-        load_weight_scales(1)
         load_resid(0, (slice(0, PAIR),))
+        load_weight_scales(1)
         load_weight_scales(2)
         load_weight_scales(3)
         load_heads(1)
         load_resid(0, (slice(PAIR, QUAD),))
-        nc.sync.dma_start(out=gain_rows[0:1, 0, :], in_=ln_gamma.unsqueeze(0))
-        nc.sync.dma_start(out=gain_rows[0:1, 1, :], in_=ln_beta.unsqueeze(0))
         load_heads(2)
         load_resid(1)
         load_heads(3)
@@ -327,22 +328,25 @@ def tile_selfattention_pa_t_kernel(tc, h_attn, x, out_w_words, out_w_scales, ln_
         for half in BOTH_PAIRS:
             flip(0, (half,))
             regroup(0, (half,))
-        for half in BOTH_PAIRS:
-            quantise(0, slice(half * PAIR, (half + 1) * PAIR))
-            project(0, (half * PAIR, half * PAIR + 1))
-        flip(1)
-        regroup(1, BOTH_PAIRS)
         gamma_all = gain_banks.tile([P, E], F32)
         nc.tensor.matmul(out=gamma_all[:], lhsT=ones[:], rhs=gain_rows[:, 0, :], start=True, stop=True)
         beta_bank = gain_banks.tile([P, E], F32)
         nc.tensor.matmul(out=beta_bank[:], lhsT=ones[:], rhs=gain_rows[:, 1, :], start=True, stop=True)
         gamma_row = keep.tile([P, E], F32)
-        beta_row = keep.tile([P, E], F32)
-
-        step(0)
         nc.scalar.copy(out=gamma_row[:], in_=gamma_all[:])
+        beta_row = keep.tile([P, E], F32)
         nc.scalar.copy(out=beta_row[:], in_=beta_bank[:])
-        for n in range(1, N_QUADS - 1):
+        quantise(0, slice(0 * PAIR, 0 * PAIR + PAIR))
+        project(0, (0, 1))
+        quantise(0, slice(1 * PAIR, 1 * PAIR + PAIR))
+        project(0, (2, 3))
+        ask_ahead(0)
+        add_residual(quad_tiles(0))
+        flip(1)
+        regroup(1, (0,))
+        regroup(1, (1,), nc.vector.tensor_copy)
+
+        for n in range(N_QUADS - 1):
             step(n)
 
         n = N_QUADS - 1

@@ -44,7 +44,7 @@ def tile_selfattention_pa_t_kernel(tc, h_attn, x, out_w_words, out_w_scales, ln_
         work = ctx.enter_context(tc.tile_pool(name="work", bufs=2))
         grouped_rows = ctx.enter_context(tc.tile_pool(name="grouped_rows", bufs=3))
         sums_rows = ctx.enter_context(tc.tile_pool(name="sums_rows", bufs=3))
-        out_rows = ctx.enter_context(tc.tile_pool(name="out_rows", bufs=8))
+        out_rows = ctx.enter_context(tc.tile_pool(name="out_rows", bufs=N_QUADS))
         stats = ctx.enter_context(tc.tile_pool(name="stats", bufs=5))
         gain_banks = ctx.enter_context(tc.psum_pool(name="gain_banks", bufs=1))
         flip_banks = ctx.enter_context(tc.psum_pool(name="flip_banks", bufs=2))
@@ -203,10 +203,9 @@ def tile_selfattention_pa_t_kernel(tc, h_attn, x, out_w_words, out_w_scales, ln_
                 out=t_at(j), in0=y_at(j), scalar=stat("neg_mean", j), in1=gamma_all[:], op0=ALU.add, op1=ALU.mult
             )
 
-        def finish(j):
-            nc.vector.scalar_tensor_tensor(
-                out=t_at(j), in0=t_at(j), scalar=stat("rstd", j), in1=beta_bank[:], op0=ALU.mult, op1=ALU.add
-            )
+        def finish(j, start=0):
+            some = t_at(j)[:, start:E]
+            nc.vector.scalar_tensor_tensor(out=some, in0=some, scalar=stat("rstd", j), in1=beta_bank[:, start:E], op0=ALU.mult, op1=ALU.add)
 
         def scale(j):
             nc.scalar.activation(out=t_at(j), in_=t_at(j), func=ACT.Copy, scale=stat("rstd", j))
@@ -252,9 +251,14 @@ def tile_selfattention_pa_t_kernel(tc, h_attn, x, out_w_words, out_w_scales, ln_
                 add_residual(quad_tiles(n))
             negate_mean(group)
             quantise(n + 1)
-            if live(n + 2):
-                flip(n + 2)
-            project(n + 1, (1, 0, 3, 2) if n > 0 else (0, 1, 2, 3))
+            if n == 0:
+                flip(2, (0,))
+                project(1, (0, 1, 2, 3))
+                flip(2, (1,))
+            else:
+                if live(n + 2):
+                    flip(n + 2)
+                project(n + 1, (1, 0, 3, 2))
             if n > 0:
                 standardise(pair_of(n - 1)[1], EARLY)
                 gain(n - 1)
@@ -281,9 +285,9 @@ def tile_selfattention_pa_t_kernel(tc, h_attn, x, out_w_words, out_w_scales, ln_
                 squares_of(v[1])
             standardise(pair[0])
             standardise(pair[1], 0, EARLY)
+            inverse_deviation(v)
             if live(n + 2):
                 regroup(n + 2, (1,))
-            inverse_deviation(v)
 
         w_plane = keep.tile([P, E], U8, align_bytes=64)
         nc.vector.memset(w_plane[:].bitcast(I32), 0)
@@ -306,15 +310,15 @@ def tile_selfattention_pa_t_kernel(tc, h_attn, x, out_w_words, out_w_scales, ln_
                 in_=out_w_scales[0, 4 * quadrant : 4 * quadrant + 4, :].bitcast(I32),
             )
 
-        load_heads_by_tile(0)
-        nc.sync.dma_start(out=gain_rows[0:1, 0, :], in_=ln_gamma.unsqueeze(0))
-        nc.sync.dma_start(out=gain_rows[0:1, 1, :], in_=ln_beta.unsqueeze(0))
         nc.sync.dma_start(out=w_words[:].bitcast(I32), in_=out_w_words[0].bitcast(I32))
         load_weight_scales(0)
-        load_resid(0, (slice(0, PAIR),))
         load_weight_scales(1)
         load_weight_scales(2)
+        load_heads_by_tile(0)
         load_weight_scales(3)
+        load_resid(0, (slice(0, PAIR),))
+        nc.sync.dma_start(out=gain_rows[0:1, 0, :], in_=ln_gamma.unsqueeze(0))
+        nc.sync.dma_start(out=gain_rows[0:1, 1, :], in_=ln_beta.unsqueeze(0))
         load_heads(1)
         load_resid(0, (slice(PAIR, QUAD),))
         load_heads(2)
@@ -337,9 +341,9 @@ def tile_selfattention_pa_t_kernel(tc, h_attn, x, out_w_words, out_w_scales, ln_
         beta_row = keep.tile([P, E], F32)
         nc.scalar.copy(out=beta_row[:], in_=beta_bank[:])
         quantise(0, slice(0 * PAIR, 0 * PAIR + PAIR))
-        project(0, (0, 1))
+        project(0, (0 * PAIR, 0 * PAIR + 1))
         quantise(0, slice(1 * PAIR, 1 * PAIR + PAIR))
-        project(0, (2, 3))
+        project(0, (1 * PAIR, 1 * PAIR + 1))
         ask_ahead(0)
         add_residual(quad_tiles(0))
         flip(1)
@@ -351,45 +355,49 @@ def tile_selfattention_pa_t_kernel(tc, h_attn, x, out_w_words, out_w_scales, ln_
 
         n = N_QUADS - 1
         group, pair = group_tiles(n), pair_of(n)
-        third, end = pair[1] + 1, N_TILES - 1
+        before, third, end = group[0], pair[1] + 1, N_TILES - 1
+        late = vector_tiles(n - 1)
         standardise(pair_of(n - 1)[1], EARLY)
-        add_residual(quad_tiles(n))
-        negate_mean(group)
         gain(n - 1)
         for a in range(PAIR):
             offset(n - 1, slice(a, a + 1))
+        negate_mean([before])
+        squares_of(before)
+        add_residual(pair)
+        negate_mean(pair)
+        squares_of(pair[0])
+        inverse_deviation([before])
+        for j in late:
+            finish(j)
+        store(late[0] - 1)
+        centre_and_gain(before)
+        add_residual([third])
         offset_rest(n - 2)
         store(pair_of(n - 2)[0])
-        for j in vector_tiles(n - 1):
-            finish(j)
-            if j % QUAD == QUAD - 1:
-                store(j - 1)
-        squares_of(group[0])
-        squares_of(pair[0])
-        inverse_deviation(group[0:1])
+        add_residual([end])
         squares_of(pair[1])
+        negate_mean([third])
         inverse_deviation(pair)
         negate_mean([end])
+        finish(before)
+        store(before - 1)
         centre_and_gain(pair[0])
-        centre_and_gain(group[0])
         centre_and_gain(pair[1])
         squares_of(third)
         scale(pair[0])
         squares_of(end)
         inverse_deviation([third])
         offset(n, slice(0, 1), E)
-        finish(group[0])
-        store(group[0] - 1)
         offset_rest(n - 1)
         store(pair_of(n - 1)[0], 1)
         finish(pair[1])
-        store(pair_of(n - 1)[1], 1)
         store(pair[1], 1)
+        store(pair_of(n - 1)[1], 1)
         centre_and_gain(third)
         inverse_deviation([end])
         centre_and_gain(end)
         finish(third)
         store(third, 1)
         finish(end)
-        store(pair[0], 1)
         store(end, 1)
+        store(pair[0], 1)

@@ -203,9 +203,10 @@ def tile_selfattention_pa_t_kernel(tc, h_attn, x, out_w_words, out_w_scales, ln_
                 out=t_at(j), in0=y_at(j), scalar=stat("neg_mean", j), in1=gamma_all[:], op0=ALU.add, op1=ALU.mult
             )
 
-        def finish(j, start=0):
-            some = t_at(j)[:, start:E]
-            nc.vector.scalar_tensor_tensor(out=some, in0=some, scalar=stat("rstd", j), in1=beta_bank[:, start:E], op0=ALU.mult, op1=ALU.add)
+        def finish(j):
+            nc.vector.scalar_tensor_tensor(
+                out=t_at(j), in0=t_at(j), scalar=stat("rstd", j), in1=beta_bank[:], op0=ALU.mult, op1=ALU.add
+            )
 
         def scale(j):
             nc.scalar.activation(out=t_at(j), in_=t_at(j), func=ACT.Copy, scale=stat("rstd", j))
@@ -310,15 +311,15 @@ def tile_selfattention_pa_t_kernel(tc, h_attn, x, out_w_words, out_w_scales, ln_
                 in_=out_w_scales[0, 4 * quadrant : 4 * quadrant + 4, :].bitcast(I32),
             )
 
-        nc.sync.dma_start(out=w_words[:].bitcast(I32), in_=out_w_words[0].bitcast(I32))
-        load_weight_scales(0)
-        load_weight_scales(1)
-        load_weight_scales(2)
         load_heads_by_tile(0)
-        load_weight_scales(3)
-        load_resid(0, (slice(0, PAIR),))
         nc.sync.dma_start(out=gain_rows[0:1, 0, :], in_=ln_gamma.unsqueeze(0))
         nc.sync.dma_start(out=gain_rows[0:1, 1, :], in_=ln_beta.unsqueeze(0))
+        nc.sync.dma_start(out=w_words[:].bitcast(I32), in_=out_w_words[0].bitcast(I32))
+        load_weight_scales(0)
+        load_resid(0, (slice(0, PAIR),))
+        load_weight_scales(1)
+        load_weight_scales(2)
+        load_weight_scales(3)
         load_heads(1)
         load_resid(0, (slice(PAIR, QUAD),))
         load_heads(2)

from contextlib import ExitStack

import concourse.mybir as mybir
from concourse.masks import make_identity

F32 = mybir.dt.float32
BF16 = mybir.dt.bfloat16
I32 = mybir.dt.int32
U32 = mybir.dt.uint32
U8 = mybir.dt.uint8
FP8X4 = mybir.dt.float8_e4m3fn_x4
FP4X4 = mybir.dt.float4_e2m1fn_x4
ALU = mybir.AluOpType
ACT = mybir.ActivationFunctionType

B, H, S, D = 4, 4, 2048, 128
E = H * D
P = 128
PACK = 4
LN_EPS = 1e-6

QUAD = 4
QUAD_TOKENS = P * QUAD
N_QUADS = B * S // QUAD_TOKENS
PAIR = 2
BOTH_PAIRS = (0, 1)
N_TILES = N_QUADS * QUAD
COLUMN = {3: 0, 2: 1, 0: 2, 1: 3}
HEADS_AHEAD = 6
RESID_AHEAD = 4
KEPT = E - 32
EARLY = E - 128

FLOPS = 2 * B * S * E * E


def tile_selfattention_pa_t_kernel(tc, h_attn, x, out_w_words, out_w_scales, ln_gamma, ln_beta, out):
    nc = tc.nc
    with ExitStack() as ctx:
        ctx.enter_context(tc.manual_schedule())
        keep = ctx.enter_context(tc.tile_pool(name="keep", bufs=1))
        heads_in = ctx.enter_context(tc.tile_pool(name="heads_in", bufs=HEADS_AHEAD - 2))
        resid_in = ctx.enter_context(tc.tile_pool(name="resid_in", bufs=RESID_AHEAD + 1))
        work = ctx.enter_context(tc.tile_pool(name="work", bufs=2))
        grouped_rows = ctx.enter_context(tc.tile_pool(name="grouped_rows", bufs=3))
        sums_rows = ctx.enter_context(tc.tile_pool(name="sums_rows", bufs=3))
        out_rows = ctx.enter_context(tc.tile_pool(name="out_rows", bufs=N_QUADS))
        stats = ctx.enter_context(tc.tile_pool(name="stats", bufs=5))
        gain_banks = ctx.enter_context(tc.psum_pool(name="gain_banks", bufs=1))
        flip_banks = ctx.enter_context(tc.psum_pool(name="flip_banks", bufs=2))
        acc_banks = ctx.enter_context(tc.psum_pool(name="acc_banks", bufs=4))

        merged_of, resid_of, flipped_of, grouped_of, codes_of, plane_of = {}, {}, {}, {}, {}, {}
        acc_of, y_of, t_of, stats_of = {}, {}, {}, {}

        def live(i):
            return 0 <= i < N_QUADS

        def token_rows(dram_2d, i):
            b, s0 = divmod(i * QUAD_TOKENS, S)
            return dram_2d[b, s0 : s0 + QUAD_TOKENS, :].rearrange("(p a) e -> p a e", a=QUAD)

        def load_heads(i):
            b, s0 = divmod(i * QUAD_TOKENS, S)
            merged = heads_in.tile([P, QUAD, E], BF16, name="merged")
            for h in range(H):
                nc.sync.dma_start(
                    out=merged[:, :, h * D : (h + 1) * D],
                    in_=h_attn[b, h, s0 : s0 + QUAD_TOKENS, :].rearrange("(p a) d -> p a d", a=QUAD),
                )
            merged_of[i] = merged

        def load_heads_by_tile(i):
            b, s0 = divmod(i * QUAD_TOKENS, S)
            merged = heads_in.tile([P, QUAD, E], BF16, name="merged")
            tokens = h_attn[b, :, s0 : s0 + QUAD_TOKENS, :].rearrange("h (p a) d -> p a h d", a=QUAD)
            for a in range(QUAD):
                nc.sync.dma_start(out=merged[:, a, :].rearrange("p (h d) -> p h d", h=H), in_=tokens[:, a, :, :])
            merged_of[i] = merged

        def load_resid(i, parts=(slice(0, QUAD),)):
            if i not in resid_of:
                resid_of[i] = resid_in.tile([P, QUAD, E], BF16, name="resid")
            for tiles in parts:
                nc.sync.dma_start(out=resid_of[i][:, tiles, :], in_=token_rows(x, i)[:, tiles, :])

        def flip(i, pairs=BOTH_PAIRS):
            words = merged_of[i][:].bitcast(F32)
            flipped_of.setdefault(i, [])
            for pair in pairs:
                flipped = flip_banks.tile([P, PAIR, 2, P], F32, name="flipped")
                for a in range(PAIR):
                    for u in range(2):
                        nc.tensor.transpose(flipped[:, a, u, :], words[:, pair * PAIR + a, u : E // 2 : 2], ident[:])
                flipped_of[i].append(flipped)

        def regroup(i, pairs, copy=nc.scalar.copy):
            if i not in grouped_of:
                grouped_of[i] = grouped_rows.tile([P, QUAD, P, PACK], BF16, align_bytes=64, name="grouped")
            grouped_words = grouped_of[i][:].bitcast(F32)
            for pair in pairs:
                copy(
                    out=grouped_words[:, pair * PAIR : (pair + 1) * PAIR, :, :],
                    in_=flipped_of[i][pair][:].rearrange("p a u n -> p a n u"),
                )

        def quantise(i, tiles=slice(0, QUAD)):
            if i not in codes_of:
                codes_of[i] = work.tile([P, QUAD * P], U32, align_bytes=64, name="codes")
                plane_of[i] = work.tile([P, QUAD * P], U8, align_bytes=64, name="plane")
            columns = slice(tiles.start * P, tiles.stop * P)
            nc.vector.quantize_mx(
                out=codes_of[i][:, columns].bitcast(FP8X4),
                scales=plane_of[i][:, columns],
                in_=grouped_of[i][:, tiles, :, :].rearrange("p a n t -> p (a n t)"),
            )

        def project(i, tiles=(0, 1, 2, 3)):
            acc_of.setdefault(i, {})
            for a in tiles:
                acc = acc_banks.tile([P, E], F32, name="acc")
                nc.tensor.matmul_mx(
                    out=acc[:],
                    lhsT=codes_of[i][:, a * P : (a + 1) * P].bitcast(FP8X4),
                    lhsT_scale=plane_of[i][:, a * P : (a + 1) * P],
                    rhs=w_words[:].bitcast(FP4X4),
                    rhs_scale=w_plane[:],
                    start=True,
                    stop=True,
                )
                acc_of[i][a] = acc

        def group_tiles(g):
            return [j for j in range(g * QUAD - 1, (g + 1) * QUAD - 1) if 0 <= j < N_TILES]

        def stats_tile(kind, j):
            g = (j + 1) // QUAD
            if (kind, g) not in stats_of:
                stats_of[kind, g] = stats.tile([P, QUAD], F32, name=kind)
            return stats_of[kind, g]

        def stat(kind, j):
            column = COLUMN[j % QUAD]
            return stats_tile(kind, j)[:, column : column + 1]

        def some_stats(kind, tiles):
            columns = sorted(COLUMN[j % QUAD] for j in tiles)
            return stats_tile(kind, tiles[0])[:, columns[0] : columns[-1] + 1]

        def rows(store_of, pool, name, j):
            if j // QUAD not in store_of:
                store_of[j // QUAD] = pool.tile([P, QUAD, E], F32, name=name)
            return store_of[j // QUAD][:, j % QUAD, :]

        def y_at(j):
            return rows(y_of, sums_rows, "y", j)

        def t_at(j):
            return rows(t_of, out_rows, "t", j)

        def add_residual(tiles):
            for j in tiles:
                nc.vector.scalar_tensor_tensor(
                    out=y_at(j),
                    in0=acc_of[j // QUAD][j % QUAD][:],
                    scalar=1.0,
                    in1=resid_of[j // QUAD][:, j % QUAD, :],
                    op0=ALU.mult,
                    op1=ALU.add,
                    accum_out=stat("sums", j),
                )

        def negate_mean(tiles):
            nc.scalar.activation(
                out=some_stats("neg_mean", tiles), in_=some_stats("sums", tiles), func=ACT.Copy, scale=-1.0 / E
            )

        def squares_of(j):
            squares = work.tile([P, E], BF16, name="squares")
            nc.scalar.activation(
                out=squares[:], in_=y_at(j), func=ACT.Square, bias=stat("neg_mean", j), scale=1.0, accum_out=stat("sum_sq", j)
            )

        def inverse_deviation(tiles):
            nc.scalar.activation(
                out=some_stats("rstd", tiles),
                in_=some_stats("sum_sq", tiles),
                func=ACT.Abs_reciprocal_sqrt,
                bias=eps[:],
                scale=1.0 / E,
            )

        def shift_of(j):
            nc.scalar.activation(out=stat("shift", j), in_=stat("neg_mean", j), func=ACT.Copy, scale=stat("rstd", j))

        def standardise(j, start=0, stop=E):
            nc.scalar.activation(
                out=t_at(j)[:, start:stop], in_=y_at(j)[:, start:stop], func=ACT.Identity, bias=stat("shift", j), scale=stat("rstd", j)
            )

        def centre_and_gain(j):
            nc.vector.scalar_tensor_tensor(
                out=t_at(j), in0=y_at(j), scalar=stat("neg_mean", j), in1=gamma_all[:], op0=ALU.add, op1=ALU.mult
            )

        def finish(j):
            nc.vector.scalar_tensor_tensor(
                out=t_at(j), in0=t_at(j), scalar=stat("rstd", j), in1=beta_bank[:], op0=ALU.mult, op1=ALU.add
            )

        def scale(j):
            nc.scalar.activation(out=t_at(j), in_=t_at(j), func=ACT.Copy, scale=stat("rstd", j))

        def wide(row, count):
            return row.unsqueeze(1).to_broadcast([P, count, row.shape[-1]])

        def gain(i, tiles=slice(0, PAIR)):
            some = t_of[i][:, tiles, :]
            nc.gpsimd.tensor_tensor(out=some, in0=some, in1=wide(gamma_row[:], tiles.stop - tiles.start), op=ALU.mult)

        def offset(i, tiles=slice(0, PAIR), width=KEPT):
            some = t_of[i][:, tiles, 0:width]
            nc.gpsimd.tensor_tensor(out=some, in0=some, in1=wide(beta_row[:, 0:width], tiles.stop - tiles.start), op=ALU.add)

        def offset_rest(i):
            some = t_of[i][:, 0:PAIR, KEPT:E]
            nc.vector.tensor_tensor(out=some, in0=some, in1=wide(beta_bank[:, KEPT:E], PAIR), op=ALU.add)

        def store(j, count=PAIR):
            tiles = slice(j % QUAD, j % QUAD + count)
            nc.sync.dma_start(out=token_rows(out, j // QUAD)[:, tiles, :], in_=t_of[j // QUAD][:, tiles, :])

        def ask_ahead(n):
            if live(n + HEADS_AHEAD):
                load_heads(n + HEADS_AHEAD)
            if live(n + RESID_AHEAD):
                load_resid(n + RESID_AHEAD)

        def quad_tiles(n):
            return range(n * QUAD, (n + 1) * QUAD)

        def vector_tiles(g):
            return [j for j in group_tiles(g) if j % QUAD >= PAIR]

        def pair_of(n):
            return [n * QUAD, n * QUAD + 1]

        def step(n):
            group, pair = group_tiles(n), pair_of(n)
            if n > 0:
                ask_ahead(n)
                add_residual(quad_tiles(n))
            negate_mean(group)
            quantise(n + 1)
            if n == 0:
                flip(2, (0,))
                project(1, (0, 1, 2, 3))
                flip(2, (1,))
            else:
                if live(n + 2):
                    flip(n + 2)
                project(n + 1, (1, 0, 3, 2))
            if n > 0:
                standardise(pair_of(n - 1)[1], EARLY)
                gain(n - 1)
                offset(n - 1)
            if n > 1:
                offset_rest(n - 2)
                store(pair_of(n - 2)[0])
            for j in vector_tiles(n - 1):
                finish(j)
                if j % QUAD == QUAD - 1:
                    store(j - 1)
            for j in vector_tiles(n):
                centre_and_gain(j)
            for j in pair:
                squares_of(j)
            if live(n + 2):
                regroup(n + 2, (0,))
            inverse_deviation(pair)
            v = vector_tiles(n)
            squares_of(v[0])
            for j in pair:
                shift_of(j)
            if len(v) > 1:
                squares_of(v[1])
            standardise(pair[0])
            standardise(pair[1], 0, EARLY)
            inverse_deviation(v)
            if live(n + 2):
                regroup(n + 2, (1,))

        w_plane = keep.tile([P, E], U8, align_bytes=64)
        nc.vector.memset(w_plane[:].bitcast(I32), 0)
        gain_rows = keep.tile([P, 2, E], BF16)
        nc.vector.memset(gain_rows[:], 0.0)
        ones = keep.tile([P, P], BF16)
        nc.vector.memset(ones[:], 1.0)
        eps = keep.tile([P, 1], F32)
        nc.vector.memset(eps[:], LN_EPS)
        ident = keep.tile([P, P], F32)
        make_identity(nc, ident[:])
        warm = keep.tile([P, 1], F32)
        nc.scalar.activation(out=warm[:], in_=eps[:], func=ACT.Abs_reciprocal_sqrt)

        w_words = keep.tile([P, 2 * E], U8, align_bytes=64)

        def load_weight_scales(quadrant):
            nc.sync.dma_start(
                out=w_plane[32 * quadrant : 32 * quadrant + 4, :].bitcast(I32),
                in_=out_w_scales[0, 4 * quadrant : 4 * quadrant + 4, :].bitcast(I32),
            )

        load_heads_by_tile(0)
        nc.sync.dma_start(out=gain_rows[0:1, 0, :], in_=ln_gamma.unsqueeze(0))
        nc.sync.dma_start(out=gain_rows[0:1, 1, :], in_=ln_beta.unsqueeze(0))
        nc.sync.dma_start(out=w_words[:].bitcast(I32), in_=out_w_words[0].bitcast(I32))
        load_weight_scales(0)
        load_resid(0, (slice(0, PAIR),))
        load_weight_scales(1)
        load_weight_scales(2)
        load_weight_scales(3)
        load_heads(1)
        load_resid(0, (slice(PAIR, QUAD),))
        load_heads(2)
        load_resid(1)
        load_heads(3)
        load_resid(2)
        load_heads(4)
        load_resid(3)
        load_heads(5)

        for half in BOTH_PAIRS:
            flip(0, (half,))
            regroup(0, (half,))
        gamma_all = gain_banks.tile([P, E], F32)
        nc.tensor.matmul(out=gamma_all[:], lhsT=ones[:], rhs=gain_rows[:, 0, :], start=True, stop=True)
        beta_bank = gain_banks.tile([P, E], F32)
        nc.tensor.matmul(out=beta_bank[:], lhsT=ones[:], rhs=gain_rows[:, 1, :], start=True, stop=True)
        gamma_row = keep.tile([P, E], F32)
        nc.scalar.copy(out=gamma_row[:], in_=gamma_all[:])
        beta_row = keep.tile([P, E], F32)
        nc.scalar.copy(out=beta_row[:], in_=beta_bank[:])
        quantise(0, slice(0 * PAIR, 0 * PAIR + PAIR))
        project(0, (0 * PAIR, 0 * PAIR + 1))
        quantise(0, slice(1 * PAIR, 1 * PAIR + PAIR))
        project(0, (1 * PAIR, 1 * PAIR + 1))
        ask_ahead(0)
        add_residual(quad_tiles(0))
        flip(1)
        regroup(1, (0,))
        regroup(1, (1,), nc.vector.tensor_copy)

        for n in range(N_QUADS - 1):
            step(n)

        n = N_QUADS - 1
        group, pair = group_tiles(n), pair_of(n)
        before, third, end = group[0], pair[1] + 1, N_TILES - 1
        late = vector_tiles(n - 1)
        standardise(pair_of(n - 1)[1], EARLY)
        gain(n - 1)
        for a in range(PAIR):
            offset(n - 1, slice(a, a + 1))
        negate_mean([before])
        squares_of(before)
        add_residual(pair)
        negate_mean(pair)
        squares_of(pair[0])
        inverse_deviation([before])
        for j in late:
            finish(j)
        store(late[0] - 1)
        centre_and_gain(before)
        add_residual([third])
        offset_rest(n - 2)
        store(pair_of(n - 2)[0])
        add_residual([end])
        squares_of(pair[1])
        negate_mean([third])
        inverse_deviation(pair)
        negate_mean([end])
        finish(before)
        store(before - 1)
        centre_and_gain(pair[0])
        centre_and_gain(pair[1])
        squares_of(third)
        scale(pair[0])
        squares_of(end)
        inverse_deviation([third])
        offset(n, slice(0, 1), E)
        offset_rest(n - 1)
        store(pair_of(n - 1)[0], 1)
        finish(pair[1])
        store(pair[1], 1)
        store(pair_of(n - 1)[1], 1)
        centre_and_gain(third)
        inverse_deviation([end])
        centre_and_gain(end)
        finish(third)
        store(third, 1)
        finish(end)
        store(end, 1)
        store(pair[0], 1)
